import numpy as np
import ml_dtypes


def mxq(x, axis, fmt="e4m3"):
    dtype, down = {"e4m3": (ml_dtypes.float8_e4m3fn, 7), "e5m2": (ml_dtypes.float8_e5m2, 14)}[fmt]
    v = np.moveaxis(np.asarray(x, np.float32).astype(ml_dtypes.bfloat16).astype(np.float64), axis, -1)
    blocks = v.reshape(v.shape[:-1] + (-1, 32))
    amax = np.abs(blocks).max(-1, keepdims=True)
    byte = np.maximum(np.where(amax > 0, np.frexp(amax)[1] - 1 + 127, 0) - down, 1)
    scale = np.exp2(byte - 127.0)
    codes = (blocks / scale).astype(np.float32).astype(dtype).astype(np.float64)
    return np.moveaxis((codes * scale).reshape(v.shape), -1, axis)


WIDE = False


def mx_kscale(k):
    if not WIDE:
        return np.ones(k)
    levels = np.array([10, -10, 5, -5, 0])
    a = np.random.permutation(np.resize(levels, k // 512 * 4)).reshape(k // 512, 4)
    idx = np.arange(k)
    return np.exp2(a[idx // 512, idx % 128 // 32])


BF16 = ml_dtypes.bfloat16


def bf(x):
    return np.asarray(x, np.float32).astype(BF16)


def f64(x):
    return np.asarray(x).astype(np.float64)


B, C, S, SEG, HID = 8, 128, 4, 512, 512
LS = S * SEG
R = B * C
ERF_CLIP, ERF_TERMS = 6.0, 120


def erf(v):
    a = np.clip(v, -ERF_CLIP, ERF_CLIP)
    a2 = 2.0 * a * a
    term = a.copy()
    tot = a.copy()
    for n in range(1, ERF_TERMS):
        term = term * a2 / (2.0 * n + 1.0)
        tot = tot + term
    return 2.0 / np.sqrt(np.pi) * np.exp(-a * a) * tot


def gelu_erf(v):
    return 0.5 * v * (1.0 + erf(v / np.sqrt(2.0)))


def setup_inputs():
    sv = np.repeat(mx_kscale(SEG), S)
    return {"x": bf(np.random.standard_normal((B, C, LS)) * sv),
            "wes1": bf(np.random.standard_normal((HID, LS)) / np.sqrt(SEG) / sv),
            "wes2": bf(np.random.standard_normal((LS, S * HID)) * 1.5 / np.sqrt(HID)),
            "wes3": bf(np.random.standard_normal((SEG, LS)) / np.sqrt(S) / sv),
            "bias1": bf(np.random.standard_normal(S * HID) * 0.5),
            "bias2": bf(np.random.standard_normal(LS) * 0.5),
            "bias3": bf(np.random.standard_normal(SEG) * 0.5)}


def reference(x, wes1, wes2, wes3, bias1, bias2, bias3):
    xr = f64(x).reshape(R, SEG, S)
    xs = mxq(xr.transpose(2, 0, 1), 2, "e4m3")
    w1 = mxq(f64(wes1).reshape(HID, SEG, S).transpose(2, 1, 0), 1, "e4m3")
    g = gelu_erf((xs @ w1) + f64(bias1).reshape(S, 1, HID))
    w2r = f64(wes2).reshape(S, SEG, S, HID)
    w2 = np.stack([w2r[i, :, i, :] for i in range(S)]).transpose(0, 2, 1)
    mid = (mxq(g, 2, "e4m3") @ mxq(w2, 1, "e4m3")) + f64(bias2).reshape(S, 1, SEG)
    jj = np.arange(SEG)
    w3 = f64(wes3).reshape(SEG, SEG, S)[jj, jj, :]
    res = (xr * w3).sum(-1) + f64(bias3)
    out = mid + res[None, :, :]
    return out.transpose(1, 2, 0).reshape(B, C, LS)

@@ -1,0 +1,278 @@
+from contextlib import ExitStack
+
+import concourse.mybir as mybir
+from concourse.masks import make_identity
+
+F32 = mybir.dt.float32
+BF16 = mybir.dt.bfloat16
+U32 = mybir.dt.uint32
+U8 = mybir.dt.uint8
+FP8X4 = mybir.dt.float8_e4m3fn_x4
+ACT = mybir.ActivationFunctionType
+ALU = mybir.AluOpType
+
+P = 128
+PACK = 4
+PHASES = 4
+SEG = 512
+HID = 512
+ROWS = 1024
+WIDTH = PHASES * SEG
+CHUNK = 512
+N_CHUNKS = ROWS // CHUNK
+TILES_PER_CHUNK = CHUNK // P
+J_TILES = SEG // P
+H_TILES = HID // P
+BANK = 512
+
+FLOPS = 2 * 2 * PHASES * ROWS * SEG * HID
+BYTES = 2 * (ROWS * WIDTH + HID * WIDTH + PHASES * SEG * HID) + 4 * ROWS * WIDTH
+
+
+def tile_maskmlp_pa_kernel(tc, x, wes1, wes2, wes3, bias1, bias2, bias3, out):
+    nc = tc.nc
+    x_rows = x.flatten_outer_dims()
+    out_rows = out.flatten_outer_dims()
+
+    with ExitStack() as ctx:
+        const = ctx.enter_context(tc.tile_pool(name="const", bufs=1))
+        load = ctx.enter_context(tc.tile_pool(name="load", bufs=8))
+        grouped = ctx.enter_context(tc.tile_pool(name="grouped", bufs=4))
+        keep = ctx.enter_context(tc.tile_pool(name="keep", bufs=1))
+        work = ctx.enter_context(tc.tile_pool(name="work", bufs=2))
+        psum = ctx.enter_context(tc.psum_pool(name="psum", bufs=2))
+
+        ident_f32 = const.tile([P, P], F32)
+        make_identity(nc, ident_f32[:])
+        ident_bf16 = const.tile([P, P], BF16)
+        make_identity(nc, ident_bf16[:])
+
+        rows_j = const.tile([P, P], BF16)
+        nc.vector.memset(rows_j[:], 0.0)
+        nc.gpsimd.dma_start(out=rows_j[0:16, :], in_=bias2.rearrange("(a m) -> a m", m=P))
+        nc.gpsimd.dma_start(out=rows_j[16:20, :], in_=bias3.rearrange("(a m) -> a m", m=P))
+        rows_h = const.tile([P, 2 * P], BF16)
+        nc.vector.memset(rows_h[:], 0.0)
+        nc.gpsimd.dma_start(out=rows_h[0:8, :], in_=bias1.rearrange("(a m) -> a m", m=2 * P))
+
+        pitch = WIDTH + PHASES
+        wes3_flat = wes3.rearrange("a b -> (a b)")
+        w3_bf16 = const.tile([P, J_TILES, 16], BF16)
+        for jt in range(J_TILES):
+            lead = WIDTH if jt == J_TILES - 1 else 0
+            first = jt * P * pitch - lead
+            window = wes3_flat[first : first + P * pitch].rearrange("(p c) -> p c", c=pitch)
+            nc.gpsimd.dma_start(out=w3_bf16[:, jt, 0:PHASES], in_=window[:, lead : lead + PHASES])
+
+        x_codes = keep.tile([P, PHASES, ROWS], U32, align_bytes=64)
+        x_scales = keep.tile([P, PHASES, ROWS], U8, align_bytes=64)
+        w1_codes = keep.tile([P, PHASES, HID], U32, align_bytes=64)
+        w1_scales = keep.tile([P, PHASES, HID], U8, align_bytes=64)
+        w2_codes = keep.tile([P, PHASES, SEG], U32, align_bytes=64)
+        w2_scales = keep.tile([P, PHASES, SEG], U8, align_bytes=64)
+        res = keep.tile([P, J_TILES, ROWS], F32)
+
+        def empty_bank(on_vector, dst, src):
+            if on_vector:
+                nc.vector.tensor_copy(out=dst, in_=src)
+            else:
+                nc.scalar.copy(out=dst, in_=src)
+
+        def split_phases(rows_sb, pair_tiles, first_row, vector_helps):
+            words = rows_sb[:].bitcast(F32).rearrange("r (j u) -> r u j", u=2)
+            for u in range(2):
+                bank = psum.tile([P, BANK], F32, tag="bank", bufs=4)
+                for jt in range(J_TILES):
+                    nc.tensor.transpose(
+                        bank[:, jt * P : (jt + 1) * P], words[:, u, jt * P : (jt + 1) * P], ident_f32[:]
+                    )
+                empty_bank(
+                    vector_helps and u == 1,
+                    pair_tiles[u][:, :, first_row : first_row + P, :],
+                    bank[:].bitcast(BF16).rearrange("p (t r e) -> p e r t", t=J_TILES, e=2),
+                )
+
+        def quantise_phases(pair_tiles, codes, scales, cols):
+            for i in range(PHASES):
+                u, e = divmod(i, 2)
+                nc.vector.quantize_mx(
+                    out=codes[:, i, cols].bitcast(FP8X4),
+                    scales=scales[:, i, cols],
+                    in_=pair_tiles[u][:, e, :, :].rearrange("p r t -> p (r t)"),
+                )
+
+        def new_pairs(label, n_rows):
+            return [
+                grouped.tile([P, 2, n_rows, PACK], BF16, name="%s%d" % (label, u), tag="pair", align_bytes=64)
+                for u in range(2)
+            ]
+
+        def load_and_split_x(c, rl, pair_tiles, vector_helps):
+            x_sb = load.tile([P, WIDTH], BF16, tag="rows")
+            first = c * CHUNK + rl * P
+            nc.sync.dma_start(out=x_sb[:], in_=x_rows[first : first + P, :])
+            split_phases(x_sb, pair_tiles, rl * P, vector_helps)
+
+        def residual(pair_tiles, cols):
+            for k in range(PHASES):
+                u, e = divmod(k, 2)
+                for jt in range(J_TILES):
+                    term = pair_tiles[u][:, e, :, jt]
+                    if k == 0:
+                        nc.scalar.activation(
+                            out=res[:, jt, cols],
+                            in_=term,
+                            func=ACT.Identity,
+                            bias=b23[:, 16 + jt : 17 + jt],
+                            scale=w3[:, jt, 0:1],
+                        )
+                    else:
+                        nc.vector.scalar_tensor_tensor(
+                            out=res[:, jt, cols],
+                            in0=term,
+                            scalar=w3[:, jt, k : k + 1],
+                            in1=res[:, jt, cols],
+                            op0=ALU.mult,
+                            op1=ALU.add,
+                        )
+
+        def prepare_w2(i):
+            w2_sb = load.tile([P, WIDTH], BF16, tag="rows")
+            block = wes2[i * SEG : (i + 1) * SEG, i * HID : (i + 1) * HID]
+            nc.sync.dma_start(
+                out=w2_sb[:].rearrange("p (t h) -> p t h", t=J_TILES),
+                in_=block.rearrange("(t p) h -> p t h", p=P),
+            )
+            words = w2_sb[:].bitcast(F32)
+            w2_grouped = work.tile([P, SEG * PACK], BF16, align_bytes=64)
+            for half in range(2):
+                bank = psum.tile([P, BANK], F32, tag="bank", bufs=4)
+                for a in range(2):
+                    for jl in range(2):
+                        src = (2 * half + jl) * (HID // 2) + a * P
+                        dst = (2 * a + jl) * P
+                        nc.tensor.transpose(bank[:, dst : dst + P], words[:, src : src + P], ident_f32[:])
+                nc.scalar.copy(
+                    out=w2_grouped[:].bitcast(F32)[:, half * BANK : (half + 1) * BANK].rearrange(
+                        "p (j a) -> p j a", a=2
+                    ),
+                    in_=bank[:].rearrange("p (a j) -> p j a", a=2),
+                )
+            nc.vector.quantize_mx(
+                out=w2_codes[:, i, :].bitcast(FP8X4), scales=w2_scales[:, i, :], in_=w2_grouped[:]
+            )
+
+        def two_layers(i, cols, total):
+            g = work.tile([P, H_TILES, CHUNK], BF16)
+            for t in range(H_TILES):
+                a_ps = psum.tile([P, CHUNK], F32, tag="bank", bufs=4)
+                nc.tensor.matmul_mx(
+                    out=a_ps[:],
+                    lhsT=w1_codes[:, i, t * P : (t + 1) * P].bitcast(FP8X4),
+                    lhsT_scale=w1_scales[:, i, t * P : (t + 1) * P],
+                    rhs=x_codes[:, i, cols].bitcast(FP8X4),
+                    rhs_scale=x_scales[:, i, cols],
+                    start=True,
+                    stop=True,
+                )
+                nc.scalar.activation(
+                    out=g[:, t, :],
+                    in_=a_ps[:],
+                    func=ACT.Gelu,
+                    bias=b1[:, i * H_TILES + t : i * H_TILES + t + 1],
+                    scale=1.0,
+                )
+            g_grouped = work.tile([P, CHUNK, PACK], BF16, align_bytes=64)
+            nc.vector.tensor_copy(
+                out=g_grouped[:].rearrange("p (c n) t -> p c t n", n=4),
+                in_=g[:].rearrange("p t (c n) -> p c t n", n=4),
+            )
+            g_codes = work.tile([P, CHUNK], U32, align_bytes=64)
+            g_scales = work.tile([P, CHUNK], U8, align_bytes=64)
+            nc.vector.quantize_mx(
+                out=g_codes[:].bitcast(FP8X4),
+                scales=g_scales[:],
+                in_=g_grouped[:].rearrange("p r t -> p (r t)"),
+            )
+            for jt in range(J_TILES):
+                m_ps = psum.tile([P, CHUNK], F32)
+                nc.tensor.matmul_mx(
+                    out=m_ps[:],
+                    lhsT=w2_codes[:, i, jt * P : (jt + 1) * P].bitcast(FP8X4),
+                    lhsT_scale=w2_scales[:, i, jt * P : (jt + 1) * P],
+                    rhs=g_codes[:].bitcast(FP8X4),
+                    rhs_scale=g_scales[:],
+                    start=True,
+                    stop=True,
+                )
+                nc.vector.scalar_tensor_tensor(
+                    out=total[:, jt, :],
+                    in0=m_ps[:],
+                    scalar=b23[:, i * J_TILES + jt : i * J_TILES + jt + 1],
+                    in1=res[:, jt, cols],
+                    op0=ALU.add,
+                    op1=ALU.add,
+                )
+
+        def write_out(c, rl, totals, vector_helps):
+            first = c * CHUNK + rl * P
+            for half in range(2):
+                o_sb = work.tile([P, 2 * BANK], F32, bufs=4)
+                for jl in range(2):
+                    jt = 2 * half + jl
+                    o_ps = psum.tile([P, BANK], F32)
+                    for i in range(PHASES):
+                        nc.tensor.transpose(
+                            o_ps[:, i * P : (i + 1) * P], totals[i][:, jt, rl * P : (rl + 1) * P], ident_f32[:]
+                        )
+                    empty_bank(
+                        vector_helps and jl == 1,
+                        o_sb[:, jl * BANK : (jl + 1) * BANK].rearrange("p (j i) -> p j i", i=PHASES),
+                        o_ps[:].rearrange("p (i j) -> p j i", i=PHASES),
+                    )
+                nc.sync.dma_start(
+                    out=out_rows[first : first + P, half * 2 * BANK : (half + 1) * 2 * BANK], in_=o_sb[:]
+                )
+
+        w1_view = wes1.rearrange("(a m e) c -> a e m c", a=2, e=2)
+        w1_pairs = new_pairs("w1_pair", HID)
+        for t in range(H_TILES):
+            w1_sb = load.tile([P, WIDTH], BF16, tag="rows")
+            nc.sync.dma_start(out=w1_sb[:], in_=w1_view[t // 2, t % 2])
+            split_phases(w1_sb, w1_pairs, t * P, True)
+        quantise_phases(w1_pairs, w1_codes, w1_scales, slice(0, HID))
+        x_pairs = new_pairs("x_pair0_", CHUNK)
+        for rl in range(TILES_PER_CHUNK):
+            load_and_split_x(0, rl, x_pairs, True)
+
+        w3 = const.tile([P, J_TILES, PHASES], F32)
+        nc.vector.tensor_copy(out=w3[:], in_=w3_bf16[:, :, 0:PHASES])
+        cols_j = psum.tile([P, P], BF16, tag="bank", bufs=4)
+        nc.tensor.transpose(cols_j[:], rows_j[:], ident_bf16[:])
+        b23 = const.tile([P, 20], F32)
+        nc.vector.tensor_copy(out=b23[:], in_=cols_j[:, 0:20])
+        cols_h = psum.tile([P, P], F32, tag="bank", bufs=4)
+        nc.tensor.transpose(cols_h[:], rows_h[:].bitcast(F32), ident_f32[:])
+        b1 = const.tile([P, 16], F32)
+        nc.vector.tensor_copy(out=b1[:], in_=cols_h[:, 0:8].bitcast(BF16))
+
+        totals = {}
+        for c in range(N_CHUNKS):
+            cols = slice(c * CHUNK, (c + 1) * CHUNK)
+            quantise_phases(x_pairs, x_codes, x_scales, cols)
+            residual(x_pairs, cols)
+            if c + 1 < N_CHUNKS:
+                x_pairs = new_pairs("x_pair%d_" % (c + 1), CHUNK)
+            totals[c] = []
+            for i in range(PHASES):
+                if c == 0:
+                    prepare_w2(i)
+                total = work.tile([P, J_TILES, CHUNK], F32, name="total%d_%d" % (c, i), tag="total", bufs=8)
+                totals[c].append(total)
+                two_layers(i, cols, total)
+                if c + 1 < N_CHUNKS:
+                    load_and_split_x(c + 1, i, x_pairs, False)
+                if c > 0:
+                    write_out(c - 1, i, totals[c - 1], False)
+        for rl in range(TILES_PER_CHUNK):
+            write_out(N_CHUNKS - 1, rl, totals[N_CHUNKS - 1], True)

@@ -24,6 +24,7 @@ TILES_PER_CHUNK = CHUNK // P
 J_TILES = SEG // P
 H_TILES = HID // P
 BANK = 512
+BANKS = {"first": 2, "second": 4, "side": 2}
 
 FLOPS = 2 * 2 * PHASES * ROWS * SEG * HID
 BYTES = 2 * (ROWS * WIDTH + HID * WIDTH + PHASES * SEG * HID) + 4 * ROWS * WIDTH
@@ -78,10 +79,10 @@ def tile_maskmlp_pa_kernel(tc, x, wes1, wes2, wes3, bias1, bias2, bias3, out):
             else:
                 nc.scalar.copy(out=dst, in_=src)
 
-        def split_phases(rows_sb, pair_tiles, first_row, vector_helps):
+        def split_phases(rows_sb, pair_tiles, first_row, vector_helps, bank_tag):
             words = rows_sb[:].bitcast(F32).rearrange("r (j u) -> r u j", u=2)
             for u in range(2):
-                bank = psum.tile([P, BANK], F32, tag="bank", bufs=4)
+                bank = psum.tile([P, BANK], F32, tag=bank_tag, bufs=BANKS[bank_tag])
                 for jt in range(J_TILES):
                     nc.tensor.transpose(
                         bank[:, jt * P : (jt + 1) * P], words[:, u, jt * P : (jt + 1) * P], ident_f32[:]
@@ -107,11 +108,11 @@ def tile_maskmlp_pa_kernel(tc, x, wes1, wes2, wes3, bias1, bias2, bias3, out):
                 for u in range(2)
             ]
 
-        def load_and_split_x(c, rl, pair_tiles, vector_helps):
+        def load_and_split_x(c, rl, pair_tiles, vector_helps, bank_tag):
             x_sb = load.tile([P, WIDTH], BF16, tag="rows")
             first = c * CHUNK + rl * P
             nc.sync.dma_start(out=x_sb[:], in_=x_rows[first : first + P, :])
-            split_phases(x_sb, pair_tiles, rl * P, vector_helps)
+            split_phases(x_sb, pair_tiles, rl * P, vector_helps, bank_tag)
 
         def residual(pair_tiles, cols):
             for k in range(PHASES):
@@ -146,7 +147,7 @@ def tile_maskmlp_pa_kernel(tc, x, wes1, wes2, wes3, bias1, bias2, bias3, out):
             words = w2_sb[:].bitcast(F32)
             w2_grouped = work.tile([P, SEG * PACK], BF16, align_bytes=64)
             for half in range(2):
-                bank = psum.tile([P, BANK], F32, tag="bank", bufs=4)
+                bank = psum.tile([P, BANK], F32, tag="side", bufs=BANKS["side"])
                 for a in range(2):
                     for jl in range(2):
                         src = (2 * half + jl) * (HID // 2) + a * P
@@ -165,7 +166,7 @@ def tile_maskmlp_pa_kernel(tc, x, wes1, wes2, wes3, bias1, bias2, bias3, out):
         def two_layers(i, cols, total):
             g = work.tile([P, H_TILES, CHUNK], BF16)
             for t in range(H_TILES):
-                a_ps = psum.tile([P, CHUNK], F32, tag="bank", bufs=4)
+                a_ps = psum.tile([P, CHUNK], F32, tag="first", bufs=BANKS["first"])
                 nc.tensor.matmul_mx(
                     out=a_ps[:],
                     lhsT=w1_codes[:, i, t * P : (t + 1) * P].bitcast(FP8X4),
@@ -195,7 +196,7 @@ def tile_maskmlp_pa_kernel(tc, x, wes1, wes2, wes3, bias1, bias2, bias3, out):
                 in_=g_grouped[:].rearrange("p r t -> p (r t)"),
             )
             for jt in range(J_TILES):
-                m_ps = psum.tile([P, CHUNK], F32)
+                m_ps = psum.tile([P, CHUNK], F32, tag="second", bufs=BANKS["second"])
                 nc.tensor.matmul_mx(
                     out=m_ps[:],
                     lhsT=w2_codes[:, i, jt * P : (jt + 1) * P].bitcast(FP8X4),
@@ -214,13 +215,13 @@ def tile_maskmlp_pa_kernel(tc, x, wes1, wes2, wes3, bias1, bias2, bias3, out):
                     op1=ALU.add,
                 )
 
-        def write_out(c, rl, totals, vector_helps):
+        def write_out(c, rl, totals, vector_helps, bank_tag):
             first = c * CHUNK + rl * P
             for half in range(2):
                 o_sb = work.tile([P, 2 * BANK], F32, bufs=4)
                 for jl in range(2):
                     jt = 2 * half + jl
-                    o_ps = psum.tile([P, BANK], F32)
+                    o_ps = psum.tile([P, BANK], F32, tag=bank_tag, bufs=BANKS[bank_tag])
                     for i in range(PHASES):
                         nc.tensor.transpose(
                             o_ps[:, i * P : (i + 1) * P], totals[i][:, jt, rl * P : (rl + 1) * P], ident_f32[:]
@@ -239,19 +240,19 @@ def tile_maskmlp_pa_kernel(tc, x, wes1, wes2, wes3, bias1, bias2, bias3, out):
         for t in range(H_TILES):
             w1_sb = load.tile([P, WIDTH], BF16, tag="rows")
             nc.sync.dma_start(out=w1_sb[:], in_=w1_view[t // 2, t % 2])
-            split_phases(w1_sb, w1_pairs, t * P, True)
+            split_phases(w1_sb, w1_pairs, t * P, True, "second")
         quantise_phases(w1_pairs, w1_codes, w1_scales, slice(0, HID))
         x_pairs = new_pairs("x_pair0_", CHUNK)
         for rl in range(TILES_PER_CHUNK):
-            load_and_split_x(0, rl, x_pairs, True)
+            load_and_split_x(0, rl, x_pairs, True, "second")
 
         w3 = const.tile([P, J_TILES, PHASES], F32)
         nc.vector.tensor_copy(out=w3[:], in_=w3_bf16[:, :, 0:PHASES])
-        cols_j = psum.tile([P, P], BF16, tag="bank", bufs=4)
+        cols_j = psum.tile([P, P], BF16, tag="side", bufs=BANKS["side"])
         nc.tensor.transpose(cols_j[:], rows_j[:], ident_bf16[:])
         b23 = const.tile([P, 20], F32)
         nc.vector.tensor_copy(out=b23[:], in_=cols_j[:, 0:20])
-        cols_h = psum.tile([P, P], F32, tag="bank", bufs=4)
+        cols_h = psum.tile([P, P], F32, tag="side", bufs=BANKS["side"])
         nc.tensor.transpose(cols_h[:], rows_h[:].bitcast(F32), ident_f32[:])
         b1 = const.tile([P, 16], F32)
         nc.vector.tensor_copy(out=b1[:], in_=cols_h[:, 0:8].bitcast(BF16))
@@ -271,8 +272,8 @@ def tile_maskmlp_pa_kernel(tc, x, wes1, wes2, wes3, bias1, bias2, bias3, out):
                 totals[c].append(total)
                 two_layers(i, cols, total)
                 if c + 1 < N_CHUNKS:
-                    load_and_split_x(c + 1, i, x_pairs, False)
+                    load_and_split_x(c + 1, i, x_pairs, False, "side")
                 if c > 0:
-                    write_out(c - 1, i, totals[c - 1], False)
+                    write_out(c - 1, i, totals[c - 1], False, "side")
         for rl in range(TILES_PER_CHUNK):
-            write_out(N_CHUNKS - 1, rl, totals[N_CHUNKS - 1], True)
+            write_out(N_CHUNKS - 1, rl, totals[N_CHUNKS - 1], True, "second")

@@ -24,7 +24,7 @@ TILES_PER_CHUNK = CHUNK // P
 J_TILES = SEG // P
 H_TILES = HID // P
 BANK = 512
-BANKS = {"first": 2, "second": 4, "side": 2}
+BANKS = {"first": 3, "second": 3, "side": 2}
 
 FLOPS = 2 * 2 * PHASES * ROWS * SEG * HID
 BYTES = 2 * (ROWS * WIDTH + HID * WIDTH + PHASES * SEG * HID) + 4 * ROWS * WIDTH
@@ -48,22 +48,9 @@ def tile_maskmlp_pa_kernel(tc, x, wes1, wes2, wes3, bias1, bias2, bias3, out):
         ident_bf16 = const.tile([P, P], BF16)
         make_identity(nc, ident_bf16[:])
 
-        rows_j = const.tile([P, P], BF16)
-        nc.vector.memset(rows_j[:], 0.0)
-        nc.gpsimd.dma_start(out=rows_j[0:16, :], in_=bias2.rearrange("(a m) -> a m", m=P))
-        nc.gpsimd.dma_start(out=rows_j[16:20, :], in_=bias3.rearrange("(a m) -> a m", m=P))
-        rows_h = const.tile([P, 2 * P], BF16)
-        nc.vector.memset(rows_h[:], 0.0)
-        nc.gpsimd.dma_start(out=rows_h[0:8, :], in_=bias1.rearrange("(a m) -> a m", m=2 * P))
-
-        pitch = WIDTH + PHASES
-        wes3_flat = wes3.rearrange("a b -> (a b)")
-        w3_bf16 = const.tile([P, J_TILES, 16], BF16)
-        for jt in range(J_TILES):
-            lead = WIDTH if jt == J_TILES - 1 else 0
-            first = jt * P * pitch - lead
-            window = wes3_flat[first : first + P * pitch].rearrange("(p c) -> p c", c=pitch)
-            nc.gpsimd.dma_start(out=w3_bf16[:, jt, 0:PHASES], in_=window[:, lead : lead + PHASES])
+        warm = const.tile([P, 2], F32)
+        nc.vector.memset(warm[:], 0.0)
+        nc.scalar.activation(out=warm[:, 1:2], in_=warm[:, 0:1], func=ACT.Gelu)
 
         x_codes = keep.tile([P, PHASES, ROWS], U32, align_bytes=64)
         x_scales = keep.tile([P, PHASES, ROWS], U8, align_bytes=64)
@@ -79,9 +66,10 @@ def tile_maskmlp_pa_kernel(tc, x, wes1, wes2, wes3, bias1, bias2, bias3, out):
             else:
                 nc.scalar.copy(out=dst, in_=src)
 
-        def split_phases(rows_sb, pair_tiles, first_row, vector_helps, bank_tag):
+        def split_phases(rows_sb, pair_tiles, first_row, vector_helps):
             words = rows_sb[:].bitcast(F32).rearrange("r (j u) -> r u j", u=2)
             for u in range(2):
+                bank_tag = ("first", "second")[u] if vector_helps else "side"
                 bank = psum.tile([P, BANK], F32, tag=bank_tag, bufs=BANKS[bank_tag])
                 for jt in range(J_TILES):
                     nc.tensor.transpose(
@@ -108,11 +96,11 @@ def tile_maskmlp_pa_kernel(tc, x, wes1, wes2, wes3, bias1, bias2, bias3, out):
                 for u in range(2)
             ]
 
-        def load_and_split_x(c, rl, pair_tiles, vector_helps, bank_tag):
+        def load_and_split_x(c, rl, pair_tiles, vector_helps):
             x_sb = load.tile([P, WIDTH], BF16, tag="rows")
             first = c * CHUNK + rl * P
             nc.sync.dma_start(out=x_sb[:], in_=x_rows[first : first + P, :])
-            split_phases(x_sb, pair_tiles, rl * P, vector_helps, bank_tag)
+            split_phases(x_sb, pair_tiles, rl * P, vector_helps)
 
         def residual(pair_tiles, cols):
             for k in range(PHASES):
@@ -215,12 +203,13 @@ def tile_maskmlp_pa_kernel(tc, x, wes1, wes2, wes3, bias1, bias2, bias3, out):
                     op1=ALU.add,
                 )
 
-        def write_out(c, rl, totals, vector_helps, bank_tag):
+        def write_out(c, rl, totals, vector_helps):
             first = c * CHUNK + rl * P
             for half in range(2):
                 o_sb = work.tile([P, 2 * BANK], F32, bufs=4)
                 for jl in range(2):
                     jt = 2 * half + jl
+                    bank_tag = ("first", "second")[jl] if vector_helps else "side"
                     o_ps = psum.tile([P, BANK], F32, tag=bank_tag, bufs=BANKS[bank_tag])
                     for i in range(PHASES):
                         nc.tensor.transpose(
@@ -239,12 +228,32 @@ def tile_maskmlp_pa_kernel(tc, x, wes1, wes2, wes3, bias1, bias2, bias3, out):
         w1_pairs = new_pairs("w1_pair", HID)
         for t in range(H_TILES):
             w1_sb = load.tile([P, WIDTH], BF16, tag="rows")
-            nc.sync.dma_start(out=w1_sb[:], in_=w1_view[t // 2, t % 2])
-            split_phases(w1_sb, w1_pairs, t * P, True, "second")
+            pieces = J_TILES if t == 0 else 1
+            for cut in range(pieces):
+                part = slice(cut * WIDTH // pieces, (cut + 1) * WIDTH // pieces)
+                nc.sync.dma_start(out=w1_sb[:, part], in_=w1_view[t // 2, t % 2][:, part])
+            split_phases(w1_sb, w1_pairs, t * P, True)
         quantise_phases(w1_pairs, w1_codes, w1_scales, slice(0, HID))
         x_pairs = new_pairs("x_pair0_", CHUNK)
         for rl in range(TILES_PER_CHUNK):
-            load_and_split_x(0, rl, x_pairs, True, "second")
+            load_and_split_x(0, rl, x_pairs, True)
+
+        rows_j = const.tile([P, P], BF16)
+        nc.vector.memset(rows_j[:], 0.0)
+        nc.sync.dma_start(out=rows_j[0:16, :], in_=bias2.rearrange("(a m) -> a m", m=P))
+        nc.sync.dma_start(out=rows_j[16:20, :], in_=bias3.rearrange("(a m) -> a m", m=P))
+        rows_h = const.tile([P, 2 * P], BF16)
+        nc.vector.memset(rows_h[:], 0.0)
+        nc.sync.dma_start(out=rows_h[0:8, :], in_=bias1.rearrange("(a m) -> a m", m=2 * P))
+
+        pitch = WIDTH + PHASES
+        wes3_flat = wes3.rearrange("a b -> (a b)")
+        w3_bf16 = const.tile([P, J_TILES, 16], BF16)
+        for jt in range(J_TILES):
+            lead = WIDTH if jt == J_TILES - 1 else 0
+            first = jt * P * pitch - lead
+            window = wes3_flat[first : first + P * pitch].rearrange("(p c) -> p c", c=pitch)
+            nc.sync.dma_start(out=w3_bf16[:, jt, 0:PHASES], in_=window[:, lead : lead + PHASES])
 
         w3 = const.tile([P, J_TILES, PHASES], F32)
         nc.vector.tensor_copy(out=w3[:], in_=w3_bf16[:, :, 0:PHASES])
@@ -272,8 +281,8 @@ def tile_maskmlp_pa_kernel(tc, x, wes1, wes2, wes3, bias1, bias2, bias3, out):
                 totals[c].append(total)
                 two_layers(i, cols, total)
                 if c + 1 < N_CHUNKS:
-                    load_and_split_x(c + 1, i, x_pairs, False, "side")
+                    load_and_split_x(c + 1, i, x_pairs, False)
                 if c > 0:
-                    write_out(c - 1, i, totals[c - 1], False, "side")
+                    write_out(c - 1, i, totals[c - 1], False)
         for rl in range(TILES_PER_CHUNK):
-            write_out(N_CHUNKS - 1, rl, totals[N_CHUNKS - 1], True, "second")
+            write_out(N_CHUNKS - 1, rl, totals[N_CHUNKS - 1], True)

@@ -172,17 +172,20 @@ def tile_maskmlp_pa_kernel(tc, x, wes1, wes2, wes3, bias1, bias2, bias3, out):
                     scale=1.0,
                 )
             g_grouped = work.tile([P, CHUNK, PACK], BF16, align_bytes=64)
-            nc.vector.tensor_copy(
-                out=g_grouped[:].rearrange("p (c n) t -> p c t n", n=4),
-                in_=g[:].rearrange("p t (c n) -> p c t n", n=4),
-            )
             g_codes = work.tile([P, CHUNK], U32, align_bytes=64)
             g_scales = work.tile([P, CHUNK], U8, align_bytes=64)
-            nc.vector.quantize_mx(
-                out=g_codes[:].bitcast(FP8X4),
-                scales=g_scales[:],
-                in_=g_grouped[:].rearrange("p r t -> p (r t)"),
-            )
+            halves = [slice(0, CHUNK // 2), slice(CHUNK // 2, CHUNK)]
+            for rows in halves:
+                nc.vector.tensor_copy(
+                    out=g_grouped[:, rows, :].rearrange("p (c n) t -> p c t n", n=4),
+                    in_=g[:, :, rows].rearrange("p t (c n) -> p c t n", n=4),
+                )
+            for rows in halves:
+                nc.vector.quantize_mx(
+                    out=g_codes[:, rows].bitcast(FP8X4),
+                    scales=g_scales[:, rows],
+                    in_=g_grouped[:, rows, :].rearrange("p r t -> p (r t)"),
+                )
             for jt in range(J_TILES):
                 m_ps = psum.tile([P, CHUNK], F32, tag="second", bufs=BANKS["second"])
                 nc.tensor.matmul_mx(

@@ -24,6 +24,7 @@ TILES_PER_CHUNK = CHUNK // P
 J_TILES = SEG // P
 H_TILES = HID // P
 BANK = 512
+VECTOR_ROWS = 384
 BANKS = {"first": 3, "second": 3, "side": 2}
 
 FLOPS = 2 * 2 * PHASES * ROWS * SEG * HID
@@ -52,8 +53,8 @@ def tile_maskmlp_pa_kernel(tc, x, wes1, wes2, wes3, bias1, bias2, bias3, out):
         nc.vector.memset(warm[:], 0.0)
         nc.scalar.activation(out=warm[:, 1:2], in_=warm[:, 0:1], func=ACT.Gelu)
 
-        x_codes = keep.tile([P, PHASES, ROWS], U32, align_bytes=64)
-        x_scales = keep.tile([P, PHASES, ROWS], U8, align_bytes=64)
+        x_codes = keep.tile([P, N_CHUNKS, PHASES, CHUNK], U32, align_bytes=64)
+        x_scales = keep.tile([P, N_CHUNKS, PHASES, CHUNK], U8, align_bytes=64)
         w1_codes = keep.tile([P, PHASES, HID], U32, align_bytes=64)
         w1_scales = keep.tile([P, PHASES, HID], U8, align_bytes=64)
         w2_codes = keep.tile([P, PHASES, SEG], U32, align_bytes=64)
@@ -81,13 +82,12 @@ def tile_maskmlp_pa_kernel(tc, x, wes1, wes2, wes3, bias1, bias2, bias3, out):
                     bank[:].bitcast(BF16).rearrange("p (t r e) -> p e r t", t=J_TILES, e=2),
                 )
 
-        def quantise_phases(pair_tiles, codes, scales, cols):
-            for i in range(PHASES):
-                u, e = divmod(i, 2)
+        def quantise_phases(pair_tiles, codes, scales):
+            for u in range(2):
                 nc.vector.quantize_mx(
-                    out=codes[:, i, cols].bitcast(FP8X4),
-                    scales=scales[:, i, cols],
-                    in_=pair_tiles[u][:, e, :, :].rearrange("p r t -> p (r t)"),
+                    out=codes[:, 2 * u : 2 * u + 2, :].rearrange("p e r -> p (e r)").bitcast(FP8X4),
+                    scales=scales[:, 2 * u : 2 * u + 2, :].rearrange("p e r -> p (e r)"),
+                    in_=pair_tiles[u][:].rearrange("p e r t -> p (e r t)"),
                 )
 
         def new_pairs(label, n_rows):
@@ -151,7 +151,7 @@ def tile_maskmlp_pa_kernel(tc, x, wes1, wes2, wes3, bias1, bias2, bias3, out):
                 out=w2_codes[:, i, :].bitcast(FP8X4), scales=w2_scales[:, i, :], in_=w2_grouped[:]
             )
 
-        def two_layers(i, cols, total):
+        def two_layers(c, i, cols, total):
             g = work.tile([P, H_TILES, CHUNK], BF16)
             for t in range(H_TILES):
                 a_ps = psum.tile([P, CHUNK], F32, tag="first", bufs=BANKS["first"])
@@ -159,8 +159,8 @@ def tile_maskmlp_pa_kernel(tc, x, wes1, wes2, wes3, bias1, bias2, bias3, out):
                     out=a_ps[:],
                     lhsT=w1_codes[:, i, t * P : (t + 1) * P].bitcast(FP8X4),
                     lhsT_scale=w1_scales[:, i, t * P : (t + 1) * P],
-                    rhs=x_codes[:, i, cols].bitcast(FP8X4),
-                    rhs_scale=x_scales[:, i, cols],
+                    rhs=x_codes[:, c, i, :].bitcast(FP8X4),
+                    rhs_scale=x_scales[:, c, i, :],
                     start=True,
                     stop=True,
                 )
@@ -172,20 +172,21 @@ def tile_maskmlp_pa_kernel(tc, x, wes1, wes2, wes3, bias1, bias2, bias3, out):
                     scale=1.0,
                 )
             g_grouped = work.tile([P, CHUNK, PACK], BF16, align_bytes=64)
+            nc.vector.tensor_copy(
+                out=g_grouped[:, 0:VECTOR_ROWS, :].rearrange("p (c n) t -> p c t n", n=4),
+                in_=g[:, :, 0:VECTOR_ROWS].rearrange("p t (c n) -> p c t n", n=4),
+            )
+            nc.scalar.copy(
+                out=g_grouped[:, VECTOR_ROWS:CHUNK, :].rearrange("p (c n) t -> p c t n", n=4),
+                in_=g[:, :, VECTOR_ROWS:CHUNK].rearrange("p t (c n) -> p c t n", n=4),
+            )
             g_codes = work.tile([P, CHUNK], U32, align_bytes=64)
             g_scales = work.tile([P, CHUNK], U8, align_bytes=64)
-            halves = [slice(0, CHUNK // 2), slice(CHUNK // 2, CHUNK)]
-            for rows in halves:
-                nc.vector.tensor_copy(
-                    out=g_grouped[:, rows, :].rearrange("p (c n) t -> p c t n", n=4),
-                    in_=g[:, :, rows].rearrange("p t (c n) -> p c t n", n=4),
-                )
-            for rows in halves:
-                nc.vector.quantize_mx(
-                    out=g_codes[:, rows].bitcast(FP8X4),
-                    scales=g_scales[:, rows],
-                    in_=g_grouped[:, rows, :].rearrange("p r t -> p (r t)"),
-                )
+            nc.vector.quantize_mx(
+                out=g_codes[:].bitcast(FP8X4),
+                scales=g_scales[:],
+                in_=g_grouped[:].rearrange("p r t -> p (r t)"),
+            )
             for jt in range(J_TILES):
                 m_ps = psum.tile([P, CHUNK], F32, tag="second", bufs=BANKS["second"])
                 nc.tensor.matmul_mx(
@@ -236,7 +237,7 @@ def tile_maskmlp_pa_kernel(tc, x, wes1, wes2, wes3, bias1, bias2, bias3, out):
                 part = slice(cut * WIDTH // pieces, (cut + 1) * WIDTH // pieces)
                 nc.sync.dma_start(out=w1_sb[:, part], in_=w1_view[t // 2, t % 2][:, part])
             split_phases(w1_sb, w1_pairs, t * P, True)
-        quantise_phases(w1_pairs, w1_codes, w1_scales, slice(0, HID))
+        quantise_phases(w1_pairs, w1_codes, w1_scales)
         x_pairs = new_pairs("x_pair0_", CHUNK)
         for rl in range(TILES_PER_CHUNK):
             load_and_split_x(0, rl, x_pairs, True)
@@ -272,7 +273,7 @@ def tile_maskmlp_pa_kernel(tc, x, wes1, wes2, wes3, bias1, bias2, bias3, out):
         totals = {}
         for c in range(N_CHUNKS):
             cols = slice(c * CHUNK, (c + 1) * CHUNK)
-            quantise_phases(x_pairs, x_codes, x_scales, cols)
+            quantise_phases(x_pairs, x_codes[:, c], x_scales[:, c])
             residual(x_pairs, cols)
             if c + 1 < N_CHUNKS:
                 x_pairs = new_pairs("x_pair%d_" % (c + 1), CHUNK)
@@ -282,7 +283,7 @@ def tile_maskmlp_pa_kernel(tc, x, wes1, wes2, wes3, bias1, bias2, bias3, out):
                     prepare_w2(i)
                 total = work.tile([P, J_TILES, CHUNK], F32, name="total%d_%d" % (c, i), tag="total", bufs=8)
                 totals[c].append(total)
-                two_layers(i, cols, total)
+                two_layers(c, i, cols, total)
                 if c + 1 < N_CHUNKS:
                     load_and_split_x(c + 1, i, x_pairs, False)
                 if c > 0:

@@ -18,14 +18,16 @@ SEG = 512
 HID = 512
 ROWS = 1024
 WIDTH = PHASES * SEG
-CHUNK = 512
+CHUNK = 256
 N_CHUNKS = ROWS // CHUNK
-TILES_PER_CHUNK = CHUNK // P
+ROW_TILES = CHUNK // P
 J_TILES = SEG // P
 H_TILES = HID // P
 BANK = 512
-VECTOR_ROWS = 384
-BANKS = {"first": 3, "second": 3, "side": 2}
+TENSOR_TERMS = 3
+VECTOR_ROWS = 192
+GPSIMD_TILES = 2
+BANKS = {"first": 3, "second": 2, "side": 3}
 
 FLOPS = 2 * 2 * PHASES * ROWS * SEG * HID
 BYTES = 2 * (ROWS * WIDTH + HID * WIDTH + PHASES * SEG * HID) + 4 * ROWS * WIDTH
@@ -38,7 +40,7 @@ def tile_maskmlp_pa_kernel(tc, x, wes1, wes2, wes3, bias1, bias2, bias3, out):
 
     with ExitStack() as ctx:
         const = ctx.enter_context(tc.tile_pool(name="const", bufs=1))
-        load = ctx.enter_context(tc.tile_pool(name="load", bufs=8))
+        load = ctx.enter_context(tc.tile_pool(name="load", bufs=10))
         grouped = ctx.enter_context(tc.tile_pool(name="grouped", bufs=4))
         keep = ctx.enter_context(tc.tile_pool(name="keep", bufs=1))
         work = ctx.enter_context(tc.tile_pool(name="work", bufs=2))
@@ -53,13 +55,13 @@ def tile_maskmlp_pa_kernel(tc, x, wes1, wes2, wes3, bias1, bias2, bias3, out):
         nc.vector.memset(warm[:], 0.0)
         nc.scalar.activation(out=warm[:, 1:2], in_=warm[:, 0:1], func=ACT.Gelu)
 
-        x_codes = keep.tile([P, N_CHUNKS, PHASES, CHUNK], U32, align_bytes=64)
-        x_scales = keep.tile([P, N_CHUNKS, PHASES, CHUNK], U8, align_bytes=64)
         w1_codes = keep.tile([P, PHASES, HID], U32, align_bytes=64)
         w1_scales = keep.tile([P, PHASES, HID], U8, align_bytes=64)
         w2_codes = keep.tile([P, PHASES, SEG], U32, align_bytes=64)
         w2_scales = keep.tile([P, PHASES, SEG], U8, align_bytes=64)
-        res = keep.tile([P, J_TILES, ROWS], F32)
+
+        def bank(tag, shape, dtype=F32, name=None):
+            return psum.tile(shape, dtype, tag=tag, bufs=BANKS[tag], name=name or tag)
 
         def empty_bank(on_vector, dst, src):
             if on_vector:
@@ -67,180 +69,216 @@ def tile_maskmlp_pa_kernel(tc, x, wes1, wes2, wes3, bias1, bias2, bias3, out):
             else:
                 nc.scalar.copy(out=dst, in_=src)
 
-        def split_phases(rows_sb, pair_tiles, first_row, vector_helps):
+        def split_pair(rows_sb, u, pair_tile, first_row, on_vector, tag):
             words = rows_sb[:].bitcast(F32).rearrange("r (j u) -> r u j", u=2)
-            for u in range(2):
-                bank_tag = ("first", "second")[u] if vector_helps else "side"
-                bank = psum.tile([P, BANK], F32, tag=bank_tag, bufs=BANKS[bank_tag])
-                for jt in range(J_TILES):
-                    nc.tensor.transpose(
-                        bank[:, jt * P : (jt + 1) * P], words[:, u, jt * P : (jt + 1) * P], ident_f32[:]
-                    )
-                empty_bank(
-                    vector_helps and u == 1,
-                    pair_tiles[u][:, :, first_row : first_row + P, :],
-                    bank[:].bitcast(BF16).rearrange("p (t r e) -> p e r t", t=J_TILES, e=2),
+            w_ps = bank(tag, [P, BANK])
+            for jt in range(J_TILES):
+                nc.tensor.transpose(
+                    w_ps[:, jt * P : (jt + 1) * P], words[:, u, jt * P : (jt + 1) * P], ident_f32[:]
                 )
+            empty_bank(
+                on_vector,
+                pair_tile[:, :, first_row : first_row + P, :],
+                w_ps[:].bitcast(BF16).rearrange("p (t r e) -> p e r t", t=J_TILES, e=2),
+            )
 
-        def quantise_phases(pair_tiles, codes, scales):
-            for u in range(2):
-                nc.vector.quantize_mx(
-                    out=codes[:, 2 * u : 2 * u + 2, :].rearrange("p e r -> p (e r)").bitcast(FP8X4),
-                    scales=scales[:, 2 * u : 2 * u + 2, :].rearrange("p e r -> p (e r)"),
-                    in_=pair_tiles[u][:].rearrange("p e r t -> p (e r t)"),
-                )
+        def quantise_pair(pair_tile, u, codes, scales):
+            nc.vector.quantize_mx(
+                out=codes[:, 2 * u : 2 * u + 2, :].rearrange("p e r -> p (e r)").bitcast(FP8X4),
+                scales=scales[:, 2 * u : 2 * u + 2, :].rearrange("p e r -> p (e r)"),
+                in_=pair_tile[:].rearrange("p e r t -> p (e r t)"),
+            )
 
-        def new_pairs(label, n_rows):
-            return [
-                grouped.tile([P, 2, n_rows, PACK], BF16, name="%s%d" % (label, u), tag="pair", align_bytes=64)
-                for u in range(2)
+        x_sb, x_pairs, x_codes, x_scales, term, big_r, g_codes, g_scales, o_sb = {}, {}, {}, {}, {}, {}, {}, {}, {}
+
+        def load_x(row_tile):
+            x_sb[row_tile] = load.tile([P, WIDTH], BF16, tag="rows", name="x_sb")
+            nc.sync.dma_start(out=x_sb[row_tile][:], in_=x_rows[row_tile * P : (row_tile + 1) * P, :])
+
+        def new_x(c):
+            x_pairs[c] = [
+                grouped.tile([P, 2, CHUNK, PACK], BF16, name="x_pair", tag="x_pair", align_bytes=64) for u in range(2)
             ]
+            x_codes[c] = keep.tile([P, PHASES, CHUNK], U32, name="x_codes%d" % c, align_bytes=64)
+            x_scales[c] = keep.tile([P, PHASES, CHUNK], U8, name="x_scales%d" % c, align_bytes=64)
 
-        def load_and_split_x(c, rl, pair_tiles, vector_helps):
-            x_sb = load.tile([P, WIDTH], BF16, tag="rows")
-            first = c * CHUNK + rl * P
-            nc.sync.dma_start(out=x_sb[:], in_=x_rows[first : first + P, :])
-            split_phases(x_sb, pair_tiles, rl * P, vector_helps)
+        def split_x(c, u, rl, on_vector, tag):
+            split_pair(x_sb[c * ROW_TILES + rl], u, x_pairs[c][u], rl * P, on_vector, tag)
 
-        def residual(pair_tiles, cols):
-            for k in range(PHASES):
-                u, e = divmod(k, 2)
-                for jt in range(J_TILES):
-                    term = pair_tiles[u][:, e, :, jt]
-                    if k == 0:
-                        nc.scalar.activation(
-                            out=res[:, jt, cols],
-                            in_=term,
-                            func=ACT.Identity,
-                            bias=b23[:, 16 + jt : 17 + jt],
-                            scale=w3[:, jt, 0:1],
-                        )
-                    else:
-                        nc.vector.scalar_tensor_tensor(
-                            out=res[:, jt, cols],
-                            in0=term,
-                            scalar=w3[:, jt, k : k + 1],
-                            in1=res[:, jt, cols],
-                            op0=ALU.mult,
-                            op1=ALU.add,
-                        )
+        def quantise_x(c, u):
+            quantise_pair(x_pairs[c][u], u, x_codes[c], x_scales[c])
 
-        def prepare_w2(i):
-            w2_sb = load.tile([P, WIDTH], BF16, tag="rows")
+        def last_term(c, jt):
+            if jt == 0:
+                term[c] = work.tile([P, J_TILES, CHUNK], F32, name="term")
+            nc.gpsimd.tensor_scalar(
+                out=term[c][:, jt, :],
+                in0=x_pairs[c][1][:, 1, :, jt],
+                scalar1=w3[:, jt, 3:4],
+                scalar2=0.0,
+                op0=ALU.mult,
+                op1=ALU.add,
+            )
+
+        def add_bias(c, rl):
+            row_tile = c * ROW_TILES + rl
+            rows = slice(rl * P, (rl + 1) * P)
+            big_r[row_tile] = work.tile([P, J_TILES, P, PHASES], F32, name="big_r", bufs=4)
+            r_ps = bank("side", [P, J_TILES, P])
+            for jt in range(J_TILES):
+                for k in range(TENSOR_TERMS):
+                    u, e = divmod(k, 2)
+                    nc.tensor.matmul(
+                        out=r_ps[:, jt, :],
+                        lhsT=x_pairs[c][u][:, e, rows, jt],
+                        rhs=diag[:, jt, k, :],
+                        start=(k == 0),
+                        stop=False,
+                    )
+                nc.tensor.matmul(
+                    out=r_ps[:, jt, :],
+                    lhsT=term[c][:, jt, rows],
+                    rhs=ident_f32[:],
+                    is_transpose=True,
+                    start=False,
+                    stop=True,
+                )
+            on_vector = J_TILES - GPSIMD_TILES
+            r_sb = work.tile([P, GPSIMD_TILES, P], F32, name="r_sb")
+            nc.scalar.copy(out=r_sb[:], in_=r_ps[:, on_vector:J_TILES, :])
+            for jt in range(J_TILES):
+                if jt < on_vector:
+                    engine, part = nc.vector, r_ps[:, jt, :]
+                else:
+                    engine, part = nc.gpsimd, r_sb[:, jt - on_vector, :]
+                engine.tensor_tensor(
+                    out=big_r[row_tile][:, jt, :, :],
+                    in0=bias[:, jt, :, :],
+                    in1=part.unsqueeze(2).to_broadcast([P, P, PHASES]),
+                    op=ALU.add,
+                )
+
+        def first_layer(c, i):
+            g = work.tile([P, H_TILES, CHUNK], BF16, name="g", bufs=3)
+            for half in range(2):
+                a_ps = bank("first", [P, 2, CHUNK])
+                for tl in range(2):
+                    t = 2 * half + tl
+                    nc.tensor.matmul_mx(
+                        out=a_ps[:, tl, :],
+                        lhsT=w1_codes[:, i, t * P : (t + 1) * P].bitcast(FP8X4),
+                        lhsT_scale=w1_scales[:, i, t * P : (t + 1) * P],
+                        rhs=x_codes[c][:, i, :].bitcast(FP8X4),
+                        rhs_scale=x_scales[c][:, i, :],
+                        start=True,
+                        stop=True,
+                    )
+                for tl in range(2):
+                    t = 2 * half + tl
+                    nc.scalar.activation(
+                        out=g[:, t, :],
+                        in_=a_ps[:, tl, :],
+                        func=ACT.Gelu,
+                        bias=b1[:, i * H_TILES + t : i * H_TILES + t + 1],
+                        scale=1.0,
+                    )
+            return g
+
+        def quantise_g(c, i, g):
+            g_grouped = work.tile([P, CHUNK, PACK], BF16, name="g_grouped", bufs=3, align_bytes=64)
+            for on_vector, rows in ((True, slice(0, VECTOR_ROWS)), (False, slice(VECTOR_ROWS, CHUNK))):
+                empty_bank(
+                    on_vector,
+                    g_grouped[:, rows, :].rearrange("p (c n) t -> p c t n", n=4),
+                    g[:, :, rows].rearrange("p t (c n) -> p c t n", n=4),
+                )
+            g_codes[c, i] = work.tile([P, CHUNK], U32, name="g_codes%d" % i, align_bytes=64)
+            g_scales[c, i] = work.tile([P, CHUNK], U8, name="g_scales%d" % i, align_bytes=64)
+            nc.vector.quantize_mx(
+                out=g_codes[c, i][:].bitcast(FP8X4),
+                scales=g_scales[c, i][:],
+                in_=g_grouped[:].rearrange("p r t -> p (r t)"),
+            )
+
+        def second_layer(c, rl, jt):
+            row_tile = c * ROW_TILES + rl
+            rows = slice(rl * P, (rl + 1) * P)
+            if jt == 0:
+                o_sb[row_tile] = work.tile([P, J_TILES, P, PHASES], F32, name="o_sb", bufs=3)
+            m_ps = bank("second", [P, PHASES, P])
+            for i in range(PHASES):
+                nc.tensor.matmul_mx(
+                    out=m_ps[:, i, :],
+                    lhsT=g_codes[c, i][:, rows].bitcast(FP8X4),
+                    lhsT_scale=g_scales[c, i][:, rows],
+                    rhs=w2_codes[:, i, jt * P : (jt + 1) * P].bitcast(FP8X4),
+                    rhs_scale=w2_scales[:, i, jt * P : (jt + 1) * P],
+                    start=True,
+                    stop=True,
+                )
+            nc.vector.tensor_tensor(
+                out=o_sb[row_tile][:, jt, :, :],
+                in0=m_ps[:].rearrange("p i j -> p j i"),
+                in1=big_r[row_tile][:, jt, :, :],
+                op=ALU.add,
+            )
+            if jt % 2 == 1:
+                half = jt // 2
+                nc.sync.dma_start(
+                    out=out_rows[row_tile * P : (row_tile + 1) * P, half * 2 * BANK : (half + 1) * 2 * BANK],
+                    in_=o_sb[row_tile][:, 2 * half : 2 * half + 2, :, :].rearrange("p t j i -> p (t j i)"),
+                )
+
+        def load_w2(i):
+            w2_sb[i] = load.tile([P, WIDTH], BF16, tag="rows", name="w2_sb")
             block = wes2[i * SEG : (i + 1) * SEG, i * HID : (i + 1) * HID]
             nc.sync.dma_start(
-                out=w2_sb[:].rearrange("p (t h) -> p t h", t=J_TILES),
+                out=w2_sb[i][:].rearrange("p (t h) -> p t h", t=J_TILES),
                 in_=block.rearrange("(t p) h -> p t h", p=P),
             )
-            words = w2_sb[:].bitcast(F32)
-            w2_grouped = work.tile([P, SEG * PACK], BF16, align_bytes=64)
+
+        w2_sb = {}
+
+        def prepare_w2(i):
+            words = w2_sb[i][:].bitcast(F32)
+            w2_grouped = work.tile([P, SEG * PACK], BF16, name="w2_grouped", align_bytes=64)
             for half in range(2):
-                bank = psum.tile([P, BANK], F32, tag="side", bufs=BANKS["side"])
+                w_ps = bank("side", [P, BANK])
                 for a in range(2):
                     for jl in range(2):
                         src = (2 * half + jl) * (HID // 2) + a * P
                         dst = (2 * a + jl) * P
-                        nc.tensor.transpose(bank[:, dst : dst + P], words[:, src : src + P], ident_f32[:])
+                        nc.tensor.transpose(w_ps[:, dst : dst + P], words[:, src : src + P], ident_f32[:])
                 nc.scalar.copy(
                     out=w2_grouped[:].bitcast(F32)[:, half * BANK : (half + 1) * BANK].rearrange(
                         "p (j a) -> p j a", a=2
                     ),
-                    in_=bank[:].rearrange("p (a j) -> p j a", a=2),
+                    in_=w_ps[:].rearrange("p (a j) -> p j a", a=2),
                 )
             nc.vector.quantize_mx(
                 out=w2_codes[:, i, :].bitcast(FP8X4), scales=w2_scales[:, i, :], in_=w2_grouped[:]
             )
 
-        def two_layers(c, i, cols, total):
-            g = work.tile([P, H_TILES, CHUNK], BF16)
-            for t in range(H_TILES):
-                a_ps = psum.tile([P, CHUNK], F32, tag="first", bufs=BANKS["first"])
-                nc.tensor.matmul_mx(
-                    out=a_ps[:],
-                    lhsT=w1_codes[:, i, t * P : (t + 1) * P].bitcast(FP8X4),
-                    lhsT_scale=w1_scales[:, i, t * P : (t + 1) * P],
-                    rhs=x_codes[:, c, i, :].bitcast(FP8X4),
-                    rhs_scale=x_scales[:, c, i, :],
-                    start=True,
-                    stop=True,
-                )
-                nc.scalar.activation(
-                    out=g[:, t, :],
-                    in_=a_ps[:],
-                    func=ACT.Gelu,
-                    bias=b1[:, i * H_TILES + t : i * H_TILES + t + 1],
-                    scale=1.0,
-                )
-            g_grouped = work.tile([P, CHUNK, PACK], BF16, align_bytes=64)
-            nc.vector.tensor_copy(
-                out=g_grouped[:, 0:VECTOR_ROWS, :].rearrange("p (c n) t -> p c t n", n=4),
-                in_=g[:, :, 0:VECTOR_ROWS].rearrange("p t (c n) -> p c t n", n=4),
-            )
-            nc.scalar.copy(
-                out=g_grouped[:, VECTOR_ROWS:CHUNK, :].rearrange("p (c n) t -> p c t n", n=4),
-                in_=g[:, :, VECTOR_ROWS:CHUNK].rearrange("p t (c n) -> p c t n", n=4),
-            )
-            g_codes = work.tile([P, CHUNK], U32, align_bytes=64)
-            g_scales = work.tile([P, CHUNK], U8, align_bytes=64)
-            nc.vector.quantize_mx(
-                out=g_codes[:].bitcast(FP8X4),
-                scales=g_scales[:],
-                in_=g_grouped[:].rearrange("p r t -> p (r t)"),
-            )
-            for jt in range(J_TILES):
-                m_ps = psum.tile([P, CHUNK], F32, tag="second", bufs=BANKS["second"])
-                nc.tensor.matmul_mx(
-                    out=m_ps[:],
-                    lhsT=w2_codes[:, i, jt * P : (jt + 1) * P].bitcast(FP8X4),
-                    lhsT_scale=w2_scales[:, i, jt * P : (jt + 1) * P],
-                    rhs=g_codes[:].bitcast(FP8X4),
-                    rhs_scale=g_scales[:],
-                    start=True,
-                    stop=True,
-                )
-                nc.vector.scalar_tensor_tensor(
-                    out=total[:, jt, :],
-                    in0=m_ps[:],
-                    scalar=b23[:, i * J_TILES + jt : i * J_TILES + jt + 1],
-                    in1=res[:, jt, cols],
-                    op0=ALU.add,
-                    op1=ALU.add,
-                )
-
-        def write_out(c, rl, totals, vector_helps):
-            first = c * CHUNK + rl * P
-            for half in range(2):
-                o_sb = work.tile([P, 2 * BANK], F32, bufs=4)
-                for jl in range(2):
-                    jt = 2 * half + jl
-                    bank_tag = ("first", "second")[jl] if vector_helps else "side"
-                    o_ps = psum.tile([P, BANK], F32, tag=bank_tag, bufs=BANKS[bank_tag])
-                    for i in range(PHASES):
-                        nc.tensor.transpose(
-                            o_ps[:, i * P : (i + 1) * P], totals[i][:, jt, rl * P : (rl + 1) * P], ident_f32[:]
-                        )
-                    empty_bank(
-                        vector_helps and jl == 1,
-                        o_sb[:, jl * BANK : (jl + 1) * BANK].rearrange("p (j i) -> p j i", i=PHASES),
-                        o_ps[:].rearrange("p (i j) -> p j i", i=PHASES),
-                    )
-                nc.sync.dma_start(
-                    out=out_rows[first : first + P, half * 2 * BANK : (half + 1) * 2 * BANK], in_=o_sb[:]
-                )
-
         w1_view = wes1.rearrange("(a m e) c -> a e m c", a=2, e=2)
-        w1_pairs = new_pairs("w1_pair", HID)
+        w1_pairs = [
+            grouped.tile([P, 2, HID, PACK], BF16, name="w1_pair%d" % u, bufs=1, align_bytes=64) for u in range(2)
+        ]
         for t in range(H_TILES):
-            w1_sb = load.tile([P, WIDTH], BF16, tag="rows")
+            w1_sb = load.tile([P, WIDTH], BF16, tag="rows", name="w1_sb")
             pieces = J_TILES if t == 0 else 1
             for cut in range(pieces):
                 part = slice(cut * WIDTH // pieces, (cut + 1) * WIDTH // pieces)
                 nc.sync.dma_start(out=w1_sb[:, part], in_=w1_view[t // 2, t % 2][:, part])
-            split_phases(w1_sb, w1_pairs, t * P, True)
-        quantise_phases(w1_pairs, w1_codes, w1_scales)
-        x_pairs = new_pairs("x_pair0_", CHUNK)
-        for rl in range(TILES_PER_CHUNK):
-            load_and_split_x(0, rl, x_pairs, True)
+            for u in range(2):
+                split_pair(w1_sb, u, w1_pairs[u], t * P, u == 1, ("first", "second")[u])
+        for rl in range(ROW_TILES):
+            load_x(rl)
+        new_x(0)
+        for u in range(2):
+            quantise_pair(w1_pairs[u], u, w1_codes, w1_scales)
+            for rl in range(ROW_TILES):
+                split_x(0, u, rl, rl == 1, ("first", "second")[rl])
+            quantise_x(0, u)
 
         rows_j = const.tile([P, P], BF16)
         nc.vector.memset(rows_j[:], 0.0)
@@ -261,32 +299,63 @@ def tile_maskmlp_pa_kernel(tc, x, wes1, wes2, wes3, bias1, bias2, bias3, out):
 
         w3 = const.tile([P, J_TILES, PHASES], F32)
         nc.vector.tensor_copy(out=w3[:], in_=w3_bf16[:, :, 0:PHASES])
-        cols_j = psum.tile([P, P], BF16, tag="side", bufs=BANKS["side"])
-        nc.tensor.transpose(cols_j[:], rows_j[:], ident_bf16[:])
-        b23 = const.tile([P, 20], F32)
-        nc.vector.tensor_copy(out=b23[:], in_=cols_j[:, 0:20])
-        cols_h = psum.tile([P, P], F32, tag="side", bufs=BANKS["side"])
+        cols_h = bank("side", [P, P])
         nc.tensor.transpose(cols_h[:], rows_h[:].bitcast(F32), ident_f32[:])
         b1 = const.tile([P, 16], F32)
         nc.vector.tensor_copy(out=b1[:], in_=cols_h[:, 0:8].bitcast(BF16))
+        cols_j = bank("side", [P, P], BF16)
+        nc.tensor.transpose(cols_j[:], rows_j[:], ident_bf16[:])
+        b2_b3 = const.tile([P, 20], F32)
+        nc.vector.tensor_copy(out=b2_b3[:], in_=cols_j[:, 0:20])
+        b23 = const.tile([P, PHASES, J_TILES], F32)
+        nc.vector.tensor_tensor(
+            out=b23[:],
+            in0=b2_b3[:, 0:16].rearrange("p (i t) -> p i t", i=PHASES),
+            in1=b2_b3[:, 16:20].unsqueeze(1).to_broadcast([P, PHASES, J_TILES]),
+            op=ALU.add,
+        )
+        diag = const.tile([P, J_TILES, TENSOR_TERMS, P], BF16)
+        nc.gpsimd.tensor_tensor(
+            out=diag[:],
+            in0=ident_bf16[:].unsqueeze(1).unsqueeze(1).to_broadcast([P, J_TILES, TENSOR_TERMS, P]),
+            in1=w3_bf16[:, :, 0:TENSOR_TERMS].unsqueeze(3).to_broadcast([P, J_TILES, TENSOR_TERMS, P]),
+            op=ALU.mult,
+        )
+        for row_tile in range(ROW_TILES, 2 * ROW_TILES):
+            load_x(row_tile)
+        for i in range(PHASES):
+            load_w2(i)
+        for row_tile in range(2 * ROW_TILES, ROWS // P):
+            load_x(row_tile)
 
-        totals = {}
-        for c in range(N_CHUNKS):
-            cols = slice(c * CHUNK, (c + 1) * CHUNK)
-            quantise_phases(x_pairs, x_codes[:, c], x_scales[:, c])
-            residual(x_pairs, cols)
-            if c + 1 < N_CHUNKS:
-                x_pairs = new_pairs("x_pair%d_" % (c + 1), CHUNK)
-            totals[c] = []
+        bias = const.tile([P, J_TILES, P, PHASES], F32)
+
+        def spread_bias(jt):
+            b_ps = bank("side", [P, PHASES, P])
             for i in range(PHASES):
+                nc.tensor.transpose(b_ps[:, i, :], b23[:, i, jt : jt + 1].to_broadcast([P, P]), ident_f32[:])
+            nc.vector.tensor_copy(out=bias[:, jt, :, :], in_=b_ps[:].rearrange("p i j -> p j i"))
+
+        for c in range(N_CHUNKS):
+            if c + 1 < N_CHUNKS:
+                new_x(c + 1)
+            for i in range(PHASES):
+                g = first_layer(c, i)
+                if c + 1 < N_CHUNKS:
+                    u, rl = divmod(i, ROW_TILES)
+                    split_x(c + 1, u, rl, False, "side")
                 if c == 0:
                     prepare_w2(i)
-                total = work.tile([P, J_TILES, CHUNK], F32, name="total%d_%d" % (c, i), tag="total", bufs=8)
-                totals[c].append(total)
-                two_layers(c, i, cols, total)
-                if c + 1 < N_CHUNKS:
-                    load_and_split_x(c + 1, i, x_pairs, False)
+                    spread_bias(i)
                 if c > 0:
-                    write_out(c - 1, i, totals[c - 1], False)
-        for rl in range(TILES_PER_CHUNK):
-            write_out(N_CHUNKS - 1, rl, totals[N_CHUNKS - 1], True)
+                    for jl in range(2):
+                        second_layer(c - 1, i // 2, (i % 2) * 2 + jl)
+                last_term(c, i)
+                quantise_g(c, i, g)
+                if c + 1 < N_CHUNKS and i % 2 == 1:
+                    quantise_x(c + 1, i // 2)
+            for rl in range(ROW_TILES):
+                add_bias(c, rl)
+        for rl in range(ROW_TILES):
+            for jt in range(J_TILES):
+                second_layer(N_CHUNKS - 1, rl, jt)

@@ -25,8 +25,8 @@ J_TILES = SEG // P
 H_TILES = HID // P
 BANK = 512
 TENSOR_TERMS = 3
-VECTOR_ROWS = 192
-GPSIMD_TILES = 2
+PAIR = 2 * CHUNK
+VECTOR_COLS = 320
 BANKS = {"first": 3, "second": 2, "side": 3}
 
 FLOPS = 2 * 2 * PHASES * ROWS * SEG * HID
@@ -89,7 +89,7 @@ def tile_maskmlp_pa_kernel(tc, x, wes1, wes2, wes3, bias1, bias2, bias3, out):
                 in_=pair_tile[:].rearrange("p e r t -> p (e r t)"),
             )
 
-        x_sb, x_pairs, x_codes, x_scales, term, big_r, g_codes, g_scales, o_sb = {}, {}, {}, {}, {}, {}, {}, {}, {}
+        x_sb, x_pairs, x_codes, x_scales, term, big_r, g_pair, g_codes, g_scales, o_sb = {}, {}, {}, {}, {}, {}, {}, {}, {}, {}
 
         def load_x(row_tile):
             x_sb[row_tile] = load.tile([P, WIDTH], BF16, tag="rows", name="x_sb")
@@ -143,23 +143,18 @@ def tile_maskmlp_pa_kernel(tc, x, wes1, wes2, wes3, bias1, bias2, bias3, out):
                     start=False,
                     stop=True,
                 )
-            on_vector = J_TILES - GPSIMD_TILES
-            r_sb = work.tile([P, GPSIMD_TILES, P], F32, name="r_sb")
-            nc.scalar.copy(out=r_sb[:], in_=r_ps[:, on_vector:J_TILES, :])
-            for jt in range(J_TILES):
-                if jt < on_vector:
-                    engine, part = nc.vector, r_ps[:, jt, :]
-                else:
-                    engine, part = nc.gpsimd, r_sb[:, jt - on_vector, :]
-                engine.tensor_tensor(
-                    out=big_r[row_tile][:, jt, :, :],
-                    in0=bias[:, jt, :, :],
-                    in1=part.unsqueeze(2).to_broadcast([P, P, PHASES]),
-                    op=ALU.add,
-                )
+            nc.vector.tensor_tensor(
+                out=big_r[row_tile][:],
+                in0=bias[:],
+                in1=r_ps[:].unsqueeze(3).to_broadcast([P, J_TILES, P, PHASES]),
+                op=ALU.add,
+            )
 
         def first_layer(c, i):
-            g = work.tile([P, H_TILES, CHUNK], BF16, name="g", bufs=3)
+            e = i % 2
+            if e == 0:
+                g_pair[c, i // 2] = work.tile([P, H_TILES, PAIR], BF16, name="g", bufs=3)
+            g = g_pair[c, i // 2]
             for half in range(2):
                 a_ps = bank("first", [P, 2, CHUNK])
                 for tl in range(2):
@@ -176,41 +171,41 @@ def tile_maskmlp_pa_kernel(tc, x, wes1, wes2, wes3, bias1, bias2, bias3, out):
                 for tl in range(2):
                     t = 2 * half + tl
                     nc.scalar.activation(
-                        out=g[:, t, :],
+                        out=g[:, t, e * CHUNK : (e + 1) * CHUNK],
                         in_=a_ps[:, tl, :],
                         func=ACT.Gelu,
                         bias=b1[:, i * H_TILES + t : i * H_TILES + t + 1],
                         scale=1.0,
                     )
-            return g
 
-        def quantise_g(c, i, g):
-            g_grouped = work.tile([P, CHUNK, PACK], BF16, name="g_grouped", bufs=3, align_bytes=64)
-            for on_vector, rows in ((True, slice(0, VECTOR_ROWS)), (False, slice(VECTOR_ROWS, CHUNK))):
+        def quantise_g(c, u):
+            g_grouped = work.tile([P, PAIR, PACK], BF16, name="g_grouped", bufs=2, align_bytes=64)
+            for on_vector, cols in ((True, slice(0, VECTOR_COLS)), (False, slice(VECTOR_COLS, PAIR))):
                 empty_bank(
                     on_vector,
-                    g_grouped[:, rows, :].rearrange("p (c n) t -> p c t n", n=4),
-                    g[:, :, rows].rearrange("p t (c n) -> p c t n", n=4),
+                    g_grouped[:, cols, :].rearrange("p (c n) t -> p c t n", n=4),
+                    g_pair[c, u][:, :, cols].rearrange("p t (c n) -> p c t n", n=4),
                 )
-            g_codes[c, i] = work.tile([P, CHUNK], U32, name="g_codes%d" % i, align_bytes=64)
-            g_scales[c, i] = work.tile([P, CHUNK], U8, name="g_scales%d" % i, align_bytes=64)
+            g_codes[c, u] = work.tile([P, PAIR], U32, name="g_codes%d" % u, align_bytes=64)
+            g_scales[c, u] = work.tile([P, PAIR], U8, name="g_scales%d" % u, align_bytes=64)
             nc.vector.quantize_mx(
-                out=g_codes[c, i][:].bitcast(FP8X4),
-                scales=g_scales[c, i][:],
+                out=g_codes[c, u][:].bitcast(FP8X4),
+                scales=g_scales[c, u][:],
                 in_=g_grouped[:].rearrange("p r t -> p (r t)"),
             )
 
         def second_layer(c, rl, jt):
             row_tile = c * ROW_TILES + rl
-            rows = slice(rl * P, (rl + 1) * P)
             if jt == 0:
                 o_sb[row_tile] = work.tile([P, J_TILES, P, PHASES], F32, name="o_sb", bufs=3)
             m_ps = bank("second", [P, PHASES, P])
             for i in range(PHASES):
+                u, e = divmod(i, 2)
+                cols = slice(e * CHUNK + rl * P, e * CHUNK + (rl + 1) * P)
                 nc.tensor.matmul_mx(
                     out=m_ps[:, i, :],
-                    lhsT=g_codes[c, i][:, rows].bitcast(FP8X4),
-                    lhsT_scale=g_scales[c, i][:, rows],
+                    lhsT=g_codes[c, u][:, cols].bitcast(FP8X4),
+                    lhsT_scale=g_scales[c, u][:, cols],
                     rhs=w2_codes[:, i, jt * P : (jt + 1) * P].bitcast(FP8X4),
                     rhs_scale=w2_scales[:, i, jt * P : (jt + 1) * P],
                     start=True,
@@ -277,7 +272,7 @@ def tile_maskmlp_pa_kernel(tc, x, wes1, wes2, wes3, bias1, bias2, bias3, out):
         for u in range(2):
             quantise_pair(w1_pairs[u], u, w1_codes, w1_scales)
             for rl in range(ROW_TILES):
-                split_x(0, u, rl, rl == 1, ("first", "second")[rl])
+                split_x(0, u, rl, rl == 1 and u == 1, ("first", "second")[rl])
             quantise_x(0, u)
 
         rows_j = const.tile([P, P], BF16)
@@ -334,13 +329,13 @@ def tile_maskmlp_pa_kernel(tc, x, wes1, wes2, wes3, bias1, bias2, bias3, out):
             b_ps = bank("side", [P, PHASES, P])
             for i in range(PHASES):
                 nc.tensor.transpose(b_ps[:, i, :], b23[:, i, jt : jt + 1].to_broadcast([P, P]), ident_f32[:])
-            nc.vector.tensor_copy(out=bias[:, jt, :, :], in_=b_ps[:].rearrange("p i j -> p j i"))
+            nc.scalar.copy(out=bias[:, jt, :, :], in_=b_ps[:].rearrange("p i j -> p j i"))
 
         for c in range(N_CHUNKS):
             if c + 1 < N_CHUNKS:
                 new_x(c + 1)
             for i in range(PHASES):
-                g = first_layer(c, i)
+                first_layer(c, i)
                 if c + 1 < N_CHUNKS:
                     u, rl = divmod(i, ROW_TILES)
                     split_x(c + 1, u, rl, False, "side")
@@ -351,9 +346,10 @@ def tile_maskmlp_pa_kernel(tc, x, wes1, wes2, wes3, bias1, bias2, bias3, out):
                     for jl in range(2):
                         second_layer(c - 1, i // 2, (i % 2) * 2 + jl)
                 last_term(c, i)
-                quantise_g(c, i, g)
-                if c + 1 < N_CHUNKS and i % 2 == 1:
-                    quantise_x(c + 1, i // 2)
+                if i % 2 == 1:
+                    quantise_g(c, i // 2)
+                    if c + 1 < N_CHUNKS:
+                        quantise_x(c + 1, i // 2)
             for rl in range(ROW_TILES):
                 add_bias(c, rl)
         for rl in range(ROW_TILES):

@@ -26,8 +26,8 @@ H_TILES = HID // P
 BANK = 512
 TENSOR_TERMS = 3
 PAIR = 2 * CHUNK
-VECTOR_COLS = 320
-BANKS = {"first": 3, "second": 2, "side": 3}
+VECTOR_ROWS = (256, 128, 0, 0)
+BANKS = {"first": 2, "second": 2, "side": 2, "rest": 2}
 
 FLOPS = 2 * 2 * PHASES * ROWS * SEG * HID
 BYTES = 2 * (ROWS * WIDTH + HID * WIDTH + PHASES * SEG * HID) + 4 * ROWS * WIDTH
@@ -69,13 +69,16 @@ def tile_maskmlp_pa_kernel(tc, x, wes1, wes2, wes3, bias1, bias2, bias3, out):
             else:
                 nc.scalar.copy(out=dst, in_=src)
 
-        def split_pair(rows_sb, u, pair_tile, first_row, on_vector, tag):
+        def transpose_pair(rows_sb, u, tag):
             words = rows_sb[:].bitcast(F32).rearrange("r (j u) -> r u j", u=2)
             w_ps = bank(tag, [P, BANK])
             for jt in range(J_TILES):
                 nc.tensor.transpose(
                     w_ps[:, jt * P : (jt + 1) * P], words[:, u, jt * P : (jt + 1) * P], ident_f32[:]
                 )
+            return w_ps
+
+        def store_pair(w_ps, pair_tile, first_row, on_vector):
             empty_bank(
                 on_vector,
                 pair_tile[:, :, first_row : first_row + P, :],
@@ -89,7 +92,8 @@ def tile_maskmlp_pa_kernel(tc, x, wes1, wes2, wes3, bias1, bias2, bias3, out):
                 in_=pair_tile[:].rearrange("p e r t -> p (e r t)"),
             )
 
-        x_sb, x_pairs, x_codes, x_scales, term, big_r, g_pair, g_codes, g_scales, o_sb = {}, {}, {}, {}, {}, {}, {}, {}, {}, {}
+        x_sb, x_ps, x_pairs, x_codes, x_scales, term, big_r = {}, {}, {}, {}, {}, {}, {}
+        a_ps, g, g_grouped, g_codes, g_scales, m_ps, o_sb = {}, {}, {}, {}, {}, {}, {}
 
         def load_x(row_tile):
             x_sb[row_tile] = load.tile([P, WIDTH], BF16, tag="rows", name="x_sb")
@@ -102,8 +106,15 @@ def tile_maskmlp_pa_kernel(tc, x, wes1, wes2, wes3, bias1, bias2, bias3, out):
             x_codes[c] = keep.tile([P, PHASES, CHUNK], U32, name="x_codes%d" % c, align_bytes=64)
             x_scales[c] = keep.tile([P, PHASES, CHUNK], U8, name="x_scales%d" % c, align_bytes=64)
 
-        def split_x(c, u, rl, on_vector, tag):
-            split_pair(x_sb[c * ROW_TILES + rl], u, x_pairs[c][u], rl * P, on_vector, tag)
+        def transpose_x(c, n):
+            u, rl = divmod(n, ROW_TILES)
+            if n == 0:
+                new_x(c)
+            x_ps[c, n] = transpose_pair(x_sb[c * ROW_TILES + rl], u, "side")
+
+        def store_x(c, n, on_vector):
+            u, rl = divmod(n, ROW_TILES)
+            store_pair(x_ps[c, n], x_pairs[c][u], rl * P, on_vector)
 
         def quantise_x(c, u):
             quantise_pair(x_pairs[c][u], u, x_codes[c], x_scales[c])
@@ -111,7 +122,7 @@ def tile_maskmlp_pa_kernel(tc, x, wes1, wes2, wes3, bias1, bias2, bias3, out):
         def last_term(c, jt):
             if jt == 0:
                 term[c] = work.tile([P, J_TILES, CHUNK], F32, name="term")
-            nc.gpsimd.tensor_scalar(
+            nc.vector.tensor_scalar(
                 out=term[c][:, jt, :],
                 in0=x_pairs[c][1][:, 1, :, jt],
                 scalar1=w3[:, jt, 3:4],
@@ -120,11 +131,9 @@ def tile_maskmlp_pa_kernel(tc, x, wes1, wes2, wes3, bias1, bias2, bias3, out):
                 op1=ALU.add,
             )
 
-        def add_bias(c, rl):
-            row_tile = c * ROW_TILES + rl
+        def sum_residual(c, rl):
             rows = slice(rl * P, (rl + 1) * P)
-            big_r[row_tile] = work.tile([P, J_TILES, P, PHASES], F32, name="big_r", bufs=4)
-            r_ps = bank("side", [P, J_TILES, P])
+            r_ps = bank("rest", [P, J_TILES, P])
             for jt in range(J_TILES):
                 for k in range(TENSOR_TERMS):
                     u, e = divmod(k, 2)
@@ -143,6 +152,11 @@ def tile_maskmlp_pa_kernel(tc, x, wes1, wes2, wes3, bias1, bias2, bias3, out):
                     start=False,
                     stop=True,
                 )
+            return r_ps
+
+        def add_bias(c, rl, r_ps):
+            row_tile = c * ROW_TILES + rl
+            big_r[row_tile] = work.tile([P, J_TILES, P, PHASES], F32, name="big_r", bufs=4)
             nc.vector.tensor_tensor(
                 out=big_r[row_tile][:],
                 in0=bias[:],
@@ -150,60 +164,64 @@ def tile_maskmlp_pa_kernel(tc, x, wes1, wes2, wes3, bias1, bias2, bias3, out):
                 op=ALU.add,
             )
 
-        def first_layer(c, i):
-            e = i % 2
+        def first_layer(s):
+            c, i = divmod(s, PHASES)
+            a_ps[s] = [bank("first", [P, 2, CHUNK]) for half in range(2)]
+            for t in range(H_TILES):
+                nc.tensor.matmul_mx(
+                    out=a_ps[s][t // 2][:, t % 2, :],
+                    lhsT=w1_codes[:, i, t * P : (t + 1) * P].bitcast(FP8X4),
+                    lhsT_scale=w1_scales[:, i, t * P : (t + 1) * P],
+                    rhs=x_codes[c][:, i, :].bitcast(FP8X4),
+                    rhs_scale=x_scales[c][:, i, :],
+                    start=True,
+                    stop=True,
+                )
+
+        def gelu(s):
+            i = s % PHASES
+            g[s] = work.tile([P, H_TILES, CHUNK], BF16, name="g", bufs=3)
+            for t in range(H_TILES):
+                nc.scalar.activation(
+                    out=g[s][:, t, :],
+                    in_=a_ps[s][t // 2][:, t % 2, :],
+                    func=ACT.Gelu,
+                    bias=b1[:, i * H_TILES + t : i * H_TILES + t + 1],
+                    scale=1.0,
+                )
+
+        def regroup(s):
+            c, i = divmod(s, PHASES)
+            u, e = divmod(i, 2)
             if e == 0:
-                g_pair[c, i // 2] = work.tile([P, H_TILES, PAIR], BF16, name="g", bufs=3)
-            g = g_pair[c, i // 2]
-            for half in range(2):
-                a_ps = bank("first", [P, 2, CHUNK])
-                for tl in range(2):
-                    t = 2 * half + tl
-                    nc.tensor.matmul_mx(
-                        out=a_ps[:, tl, :],
-                        lhsT=w1_codes[:, i, t * P : (t + 1) * P].bitcast(FP8X4),
-                        lhsT_scale=w1_scales[:, i, t * P : (t + 1) * P],
-                        rhs=x_codes[c][:, i, :].bitcast(FP8X4),
-                        rhs_scale=x_scales[c][:, i, :],
-                        start=True,
-                        stop=True,
-                    )
-                for tl in range(2):
-                    t = 2 * half + tl
-                    nc.scalar.activation(
-                        out=g[:, t, e * CHUNK : (e + 1) * CHUNK],
-                        in_=a_ps[:, tl, :],
-                        func=ACT.Gelu,
-                        bias=b1[:, i * H_TILES + t : i * H_TILES + t + 1],
-                        scale=1.0,
+                g_grouped[c, u] = work.tile([P, PAIR, PACK], BF16, name="g_grouped", bufs=2, align_bytes=64)
+            dst = g_grouped[c, u][:, e * CHUNK : (e + 1) * CHUNK, :]
+            split = VECTOR_ROWS[c]
+            for on_vector, rows in ((True, slice(0, split)), (False, slice(split, CHUNK))):
+                if rows.start < rows.stop:
+                    empty_bank(
+                        on_vector,
+                        dst[:, rows, :].rearrange("p (c n) t -> p c t n", n=4),
+                        g[s][:, :, rows].rearrange("p t (c n) -> p c t n", n=4),
                     )
 
         def quantise_g(c, u):
-            g_grouped = work.tile([P, PAIR, PACK], BF16, name="g_grouped", bufs=2, align_bytes=64)
-            for on_vector, cols in ((True, slice(0, VECTOR_COLS)), (False, slice(VECTOR_COLS, PAIR))):
-                empty_bank(
-                    on_vector,
-                    g_grouped[:, cols, :].rearrange("p (c n) t -> p c t n", n=4),
-                    g_pair[c, u][:, :, cols].rearrange("p t (c n) -> p c t n", n=4),
-                )
             g_codes[c, u] = work.tile([P, PAIR], U32, name="g_codes%d" % u, align_bytes=64)
             g_scales[c, u] = work.tile([P, PAIR], U8, name="g_scales%d" % u, align_bytes=64)
             nc.vector.quantize_mx(
                 out=g_codes[c, u][:].bitcast(FP8X4),
                 scales=g_scales[c, u][:],
-                in_=g_grouped[:].rearrange("p r t -> p (r t)"),
+                in_=g_grouped[c, u][:].rearrange("p r t -> p (r t)"),
             )
 
-        def second_layer(c, rl, jt):
-            row_tile = c * ROW_TILES + rl
-            if jt == 0:
-                o_sb[row_tile] = work.tile([P, J_TILES, P, PHASES], F32, name="o_sb", bufs=3)
-            m_ps = bank("second", [P, PHASES, P])
+        def second_layer(c, n):
+            rl, jt = divmod(n, J_TILES)
+            m_ps[c, n] = bank("second", [P, PHASES, P])
             for i in range(PHASES):
                 u, e = divmod(i, 2)
                 cols = slice(e * CHUNK + rl * P, e * CHUNK + (rl + 1) * P)
                 nc.tensor.matmul_mx(
-                    out=m_ps[:, i, :],
+                    out=m_ps[c, n][:, i, :],
                     lhsT=g_codes[c, u][:, cols].bitcast(FP8X4),
                     lhsT_scale=g_scales[c, u][:, cols],
                     rhs=w2_codes[:, i, jt * P : (jt + 1) * P].bitcast(FP8X4),
@@ -211,9 +229,15 @@ def tile_maskmlp_pa_kernel(tc, x, wes1, wes2, wes3, bias1, bias2, bias3, out):
                     start=True,
                     stop=True,
                 )
+
+        def finish(c, n):
+            rl, jt = divmod(n, J_TILES)
+            row_tile = c * ROW_TILES + rl
+            if jt == 0:
+                o_sb[row_tile] = work.tile([P, J_TILES, P, PHASES], F32, name="o_sb", bufs=3)
             nc.vector.tensor_tensor(
                 out=o_sb[row_tile][:, jt, :, :],
-                in0=m_ps[:].rearrange("p i j -> p j i"),
+                in0=m_ps[c, n][:].rearrange("p i j -> p j i"),
                 in1=big_r[row_tile][:, jt, :, :],
                 op=ALU.add,
             )
@@ -232,26 +256,31 @@ def tile_maskmlp_pa_kernel(tc, x, wes1, wes2, wes3, bias1, bias2, bias3, out):
                 in_=block.rearrange("(t p) h -> p t h", p=P),
             )
 
-        w2_sb = {}
+        w2_sb, w2_grouped = {}, {}
 
-        def prepare_w2(i):
+        def transpose_w2(i, half):
             words = w2_sb[i][:].bitcast(F32)
-            w2_grouped = work.tile([P, SEG * PACK], BF16, name="w2_grouped", align_bytes=64)
-            for half in range(2):
-                w_ps = bank("side", [P, BANK])
-                for a in range(2):
-                    for jl in range(2):
-                        src = (2 * half + jl) * (HID // 2) + a * P
-                        dst = (2 * a + jl) * P
-                        nc.tensor.transpose(w_ps[:, dst : dst + P], words[:, src : src + P], ident_f32[:])
-                nc.scalar.copy(
-                    out=w2_grouped[:].bitcast(F32)[:, half * BANK : (half + 1) * BANK].rearrange(
-                        "p (j a) -> p j a", a=2
-                    ),
-                    in_=w_ps[:].rearrange("p (a j) -> p j a", a=2),
-                )
+            w_ps = bank("side", [P, BANK])
+            for a in range(2):
+                for jl in range(2):
+                    src = (2 * half + jl) * (HID // 2) + a * P
+                    dst = (2 * a + jl) * P
+                    nc.tensor.transpose(w_ps[:, dst : dst + P], words[:, src : src + P], ident_f32[:])
+            return w_ps
+
+        def store_w2(i, half, w_ps):
+            if half == 0:
+                w2_grouped[i] = work.tile([P, SEG * PACK], BF16, name="w2_grouped", align_bytes=64)
+            nc.scalar.copy(
+                out=w2_grouped[i][:].bitcast(F32)[:, half * BANK : (half + 1) * BANK].rearrange(
+                    "p (j a) -> p j a", a=2
+                ),
+                in_=w_ps[:].rearrange("p (a j) -> p j a", a=2),
+            )
+
+        def quantise_w2(i):
             nc.vector.quantize_mx(
-                out=w2_codes[:, i, :].bitcast(FP8X4), scales=w2_scales[:, i, :], in_=w2_grouped[:]
+                out=w2_codes[:, i, :].bitcast(FP8X4), scales=w2_scales[:, i, :], in_=w2_grouped[i][:]
             )
 
         w1_view = wes1.rearrange("(a m e) c -> a e m c", a=2, e=2)
@@ -265,15 +294,15 @@ def tile_maskmlp_pa_kernel(tc, x, wes1, wes2, wes3, bias1, bias2, bias3, out):
                 part = slice(cut * WIDTH // pieces, (cut + 1) * WIDTH // pieces)
                 nc.sync.dma_start(out=w1_sb[:, part], in_=w1_view[t // 2, t % 2][:, part])
             for u in range(2):
-                split_pair(w1_sb, u, w1_pairs[u], t * P, u == 1, ("first", "second")[u])
+                store_pair(transpose_pair(w1_sb, u, ("first", "second")[u]), w1_pairs[u], t * P, u == 1)
         for rl in range(ROW_TILES):
             load_x(rl)
-        new_x(0)
-        for u in range(2):
-            quantise_pair(w1_pairs[u], u, w1_codes, w1_scales)
-            for rl in range(ROW_TILES):
-                split_x(0, u, rl, rl == 1 and u == 1, ("first", "second")[rl])
-            quantise_x(0, u)
+        quantise_pair(w1_pairs[0], 0, w1_codes, w1_scales)
+        for n in range(ROW_TILES):
+            transpose_x(0, n)
+            store_x(0, n, False)
+        quantise_x(0, 0)
+        quantise_pair(w1_pairs[1], 1, w1_codes, w1_scales)
 
         rows_j = const.tile([P, P], BF16)
         nc.vector.memset(rows_j[:], 0.0)
@@ -294,11 +323,11 @@ def tile_maskmlp_pa_kernel(tc, x, wes1, wes2, wes3, bias1, bias2, bias3, out):
 
         w3 = const.tile([P, J_TILES, PHASES], F32)
         nc.vector.tensor_copy(out=w3[:], in_=w3_bf16[:, :, 0:PHASES])
-        cols_h = bank("side", [P, P])
+        cols_h = bank("rest", [P, P])
         nc.tensor.transpose(cols_h[:], rows_h[:].bitcast(F32), ident_f32[:])
         b1 = const.tile([P, 16], F32)
         nc.vector.tensor_copy(out=b1[:], in_=cols_h[:, 0:8].bitcast(BF16))
-        cols_j = bank("side", [P, P], BF16)
+        cols_j = bank("rest", [P, P], BF16)
         nc.tensor.transpose(cols_j[:], rows_j[:], ident_bf16[:])
         b2_b3 = const.tile([P, 20], F32)
         nc.vector.tensor_copy(out=b2_b3[:], in_=cols_j[:, 0:20])
@@ -310,12 +339,16 @@ def tile_maskmlp_pa_kernel(tc, x, wes1, wes2, wes3, bias1, bias2, bias3, out):
             op=ALU.add,
         )
         diag = const.tile([P, J_TILES, TENSOR_TERMS, P], BF16)
-        nc.gpsimd.tensor_tensor(
-            out=diag[:],
-            in0=ident_bf16[:].unsqueeze(1).unsqueeze(1).to_broadcast([P, J_TILES, TENSOR_TERMS, P]),
-            in1=w3_bf16[:, :, 0:TENSOR_TERMS].unsqueeze(3).to_broadcast([P, J_TILES, TENSOR_TERMS, P]),
-            op=ALU.mult,
-        )
+        for jt in range(J_TILES):
+            for k in range(TENSOR_TERMS):
+                nc.vector.tensor_scalar(
+                    out=diag[:, jt, k, :],
+                    in0=ident_bf16[:],
+                    scalar1=w3[:, jt, k : k + 1],
+                    scalar2=0.0,
+                    op0=ALU.mult,
+                    op1=ALU.add,
+                )
         for row_tile in range(ROW_TILES, 2 * ROW_TILES):
             load_x(row_tile)
         for i in range(PHASES):
@@ -326,32 +359,51 @@ def tile_maskmlp_pa_kernel(tc, x, wes1, wes2, wes3, bias1, bias2, bias3, out):
         bias = const.tile([P, J_TILES, P, PHASES], F32)
 
         def spread_bias(jt):
-            b_ps = bank("side", [P, PHASES, P])
+            b_ps = bank("rest", [P, PHASES, P])
             for i in range(PHASES):
                 nc.tensor.transpose(b_ps[:, i, :], b23[:, i, jt : jt + 1].to_broadcast([P, P]), ident_f32[:])
-            nc.scalar.copy(out=bias[:, jt, :, :], in_=b_ps[:].rearrange("p i j -> p j i"))
+            nc.vector.tensor_copy(out=bias[:, jt, :, :], in_=b_ps[:].rearrange("p i j -> p j i"))
 
+        for n in range(ROW_TILES, 2 * ROW_TILES):
+            transpose_x(0, n)
+            store_x(0, n, False)
+        quantise_x(0, 1)
+        for jt in range(J_TILES):
+            spread_bias(jt)
+        for jt in range(J_TILES):
+            last_term(0, jt)
         for c in range(N_CHUNKS):
-            if c + 1 < N_CHUNKS:
-                new_x(c + 1)
             for i in range(PHASES):
-                first_layer(c, i)
-                if c + 1 < N_CHUNKS:
-                    u, rl = divmod(i, ROW_TILES)
-                    split_x(c + 1, u, rl, False, "side")
+                s = PHASES * c + i
+                first_layer(s)
+                gelu(s)
+                if c + 1 < N_CHUNKS and c > 0:
+                    transpose_x(c + 1, i)
+                    store_x(c + 1, i, False)
                 if c == 0:
-                    prepare_w2(i)
-                    spread_bias(i)
+                    for half in range(2):
+                        store_w2(i, half, transpose_w2(i, half))
+                    quantise_w2(i)
+                regroup(s)
                 if c > 0:
-                    for jl in range(2):
-                        second_layer(c - 1, i // 2, (i % 2) * 2 + jl)
-                last_term(c, i)
+                    for n in range(2 * i, 2 * i + 2):
+                        second_layer(c - 1, n)
+                        finish(c - 1, n)
+                if i < ROW_TILES:
+                    add_bias(c, i, sum_residual(c, i))
                 if i % 2 == 1:
                     quantise_g(c, i // 2)
-                    if c + 1 < N_CHUNKS:
+                    if c + 1 < N_CHUNKS and c > 0:
                         quantise_x(c + 1, i // 2)
-            for rl in range(ROW_TILES):
-                add_bias(c, rl)
-        for rl in range(ROW_TILES):
-            for jt in range(J_TILES):
-                second_layer(N_CHUNKS - 1, rl, jt)
+            if c == 0:
+                for n in range(PHASES):
+                    transpose_x(1, n)
+                    store_x(1, n, False)
+                    if n % 2 == 1:
+                        quantise_x(1, n // 2)
+            if c + 1 < N_CHUNKS:
+                for jt in range(J_TILES):
+                    last_term(c + 1, jt)
+        for n in range(2 * PHASES):
+            second_layer(N_CHUNKS - 1, n)
+            finish(N_CHUNKS - 1, n)

@@ -216,7 +216,7 @@ def tile_maskmlp_pa_kernel(tc, x, wes1, wes2, wes3, bias1, bias2, bias3, out):
 
         def second_layer(c, n):
             rl, jt = divmod(n, J_TILES)
-            m_ps[c, n] = bank("second", [P, PHASES, P])
+            m_ps[c, n] = bank(("second", "first")[n % 2 if c == N_CHUNKS - 1 else 0], [P, PHASES, P])
             for i in range(PHASES):
                 u, e = divmod(i, 2)
                 cols = slice(e * CHUNK + rl * P, e * CHUNK + (rl + 1) * P)
@@ -241,11 +241,12 @@ def tile_maskmlp_pa_kernel(tc, x, wes1, wes2, wes3, bias1, bias2, bias3, out):
                 in1=big_r[row_tile][:, jt, :, :],
                 op=ALU.add,
             )
-            if jt % 2 == 1:
-                half = jt // 2
+            banks = 1 if row_tile == ROWS // P - 1 else 2
+            if (jt + 1) % banks == 0:
+                tiles = slice(jt + 1 - banks, jt + 1)
                 nc.sync.dma_start(
-                    out=out_rows[row_tile * P : (row_tile + 1) * P, half * 2 * BANK : (half + 1) * 2 * BANK],
-                    in_=o_sb[row_tile][:, 2 * half : 2 * half + 2, :, :].rearrange("p t j i -> p (t j i)"),
+                    out=out_rows[row_tile * P : (row_tile + 1) * P, tiles.start * BANK : tiles.stop * BANK],
+                    in_=o_sb[row_tile][:, tiles, :, :].rearrange("p t j i -> p (t j i)"),
                 )
 
         def load_w2(i):
@@ -283,27 +284,6 @@ def tile_maskmlp_pa_kernel(tc, x, wes1, wes2, wes3, bias1, bias2, bias3, out):
                 out=w2_codes[:, i, :].bitcast(FP8X4), scales=w2_scales[:, i, :], in_=w2_grouped[i][:]
             )
 
-        w1_view = wes1.rearrange("(a m e) c -> a e m c", a=2, e=2)
-        w1_pairs = [
-            grouped.tile([P, 2, HID, PACK], BF16, name="w1_pair%d" % u, bufs=1, align_bytes=64) for u in range(2)
-        ]
-        for t in range(H_TILES):
-            w1_sb = load.tile([P, WIDTH], BF16, tag="rows", name="w1_sb")
-            pieces = J_TILES if t == 0 else 1
-            for cut in range(pieces):
-                part = slice(cut * WIDTH // pieces, (cut + 1) * WIDTH // pieces)
-                nc.sync.dma_start(out=w1_sb[:, part], in_=w1_view[t // 2, t % 2][:, part])
-            for u in range(2):
-                store_pair(transpose_pair(w1_sb, u, ("first", "second")[u]), w1_pairs[u], t * P, u == 1)
-        for rl in range(ROW_TILES):
-            load_x(rl)
-        quantise_pair(w1_pairs[0], 0, w1_codes, w1_scales)
-        for n in range(ROW_TILES):
-            transpose_x(0, n)
-            store_x(0, n, False)
-        quantise_x(0, 0)
-        quantise_pair(w1_pairs[1], 1, w1_codes, w1_scales)
-
         rows_j = const.tile([P, P], BF16)
         nc.vector.memset(rows_j[:], 0.0)
         nc.sync.dma_start(out=rows_j[0:16, :], in_=bias2.rearrange("(a m) -> a m", m=P))
@@ -322,33 +302,58 @@ def tile_maskmlp_pa_kernel(tc, x, wes1, wes2, wes3, bias1, bias2, bias3, out):
             nc.sync.dma_start(out=w3_bf16[:, jt, 0:PHASES], in_=window[:, lead : lead + PHASES])
 
         w3 = const.tile([P, J_TILES, PHASES], F32)
-        nc.vector.tensor_copy(out=w3[:], in_=w3_bf16[:, :, 0:PHASES])
-        cols_h = bank("rest", [P, P])
-        nc.tensor.transpose(cols_h[:], rows_h[:].bitcast(F32), ident_f32[:])
         b1 = const.tile([P, 16], F32)
-        nc.vector.tensor_copy(out=b1[:], in_=cols_h[:, 0:8].bitcast(BF16))
-        cols_j = bank("rest", [P, P], BF16)
-        nc.tensor.transpose(cols_j[:], rows_j[:], ident_bf16[:])
         b2_b3 = const.tile([P, 20], F32)
-        nc.vector.tensor_copy(out=b2_b3[:], in_=cols_j[:, 0:20])
         b23 = const.tile([P, PHASES, J_TILES], F32)
-        nc.vector.tensor_tensor(
-            out=b23[:],
-            in0=b2_b3[:, 0:16].rearrange("p (i t) -> p i t", i=PHASES),
-            in1=b2_b3[:, 16:20].unsqueeze(1).to_broadcast([P, PHASES, J_TILES]),
-            op=ALU.add,
-        )
         diag = const.tile([P, J_TILES, TENSOR_TERMS, P], BF16)
-        for jt in range(J_TILES):
-            for k in range(TENSOR_TERMS):
-                nc.vector.tensor_scalar(
-                    out=diag[:, jt, k, :],
-                    in0=ident_bf16[:],
-                    scalar1=w3[:, jt, k : k + 1],
-                    scalar2=0.0,
-                    op0=ALU.mult,
-                    op1=ALU.add,
-                )
+        def prepare_small():
+            nc.vector.tensor_copy(out=w3[:], in_=w3_bf16[:, :, 0:PHASES])
+            cols_h = bank("rest", [P, P])
+            nc.tensor.transpose(cols_h[:], rows_h[:].bitcast(F32), ident_f32[:])
+            nc.vector.tensor_copy(out=b1[:], in_=cols_h[:, 0:8].bitcast(BF16))
+            cols_j = bank("rest", [P, P], BF16)
+            nc.tensor.transpose(cols_j[:], rows_j[:], ident_bf16[:])
+            nc.vector.tensor_copy(out=b2_b3[:], in_=cols_j[:, 0:20])
+            nc.vector.tensor_tensor(
+                out=b23[:],
+                in0=b2_b3[:, 0:16].rearrange("p (i t) -> p i t", i=PHASES),
+                in1=b2_b3[:, 16:20].unsqueeze(1).to_broadcast([P, PHASES, J_TILES]),
+                op=ALU.add,
+            )
+            for jt in range(J_TILES):
+                for k in range(TENSOR_TERMS):
+                    nc.vector.tensor_scalar(
+                        out=diag[:, jt, k, :],
+                        in0=ident_bf16[:],
+                        scalar1=w3[:, jt, k : k + 1],
+                        scalar2=0.0,
+                        op0=ALU.mult,
+                        op1=ALU.add,
+                    )
+
+        w1_view = wes1.rearrange("(a m e) c -> a e m c", a=2, e=2)
+        w1_pairs = [
+            grouped.tile([P, 2, HID, PACK], BF16, name="w1_pair%d" % u, bufs=1, align_bytes=64) for u in range(2)
+        ]
+        for t in range(H_TILES):
+            w1_sb = load.tile([P, WIDTH], BF16, tag="rows", name="w1_sb")
+            pieces = J_TILES if t == 0 else 1
+            for cut in range(pieces):
+                part = slice(cut * WIDTH // pieces, (cut + 1) * WIDTH // pieces)
+                nc.sync.dma_start(out=w1_sb[:, part], in_=w1_view[t // 2, t % 2][:, part])
+            for u in range(2):
+                store_pair(transpose_pair(w1_sb, u, ("first", "second")[u]), w1_pairs[u], t * P, u == 1)
+            if t == 0:
+                prepare_small()
+        for rl in range(ROW_TILES):
+            load_x(rl)
+        quantise_pair(w1_pairs[0], 0, w1_codes, w1_scales)
+        for n in range(ROW_TILES):
+            transpose_x(0, n)
+            store_x(0, n, False)
+        quantise_x(0, 0)
+        quantise_pair(w1_pairs[1], 1, w1_codes, w1_scales)
+
         for row_tile in range(ROW_TILES, 2 * ROW_TILES):
             load_x(row_tile)
         for i in range(PHASES):
@@ -384,17 +389,18 @@ def tile_maskmlp_pa_kernel(tc, x, wes1, wes2, wes3, bias1, bias2, bias3, out):
                     for half in range(2):
                         store_w2(i, half, transpose_w2(i, half))
                     quantise_w2(i)
-                regroup(s)
+                if s > 0:
+                    regroup(s - 1)
+                if s >= 2 and s % 2 == 0:
+                    quantise_g((s - 2) // PHASES, (s - 2) % PHASES // 2)
                 if c > 0:
                     for n in range(2 * i, 2 * i + 2):
                         second_layer(c - 1, n)
                         finish(c - 1, n)
                 if i < ROW_TILES:
                     add_bias(c, i, sum_residual(c, i))
-                if i % 2 == 1:
-                    quantise_g(c, i // 2)
-                    if c + 1 < N_CHUNKS and c > 0:
-                        quantise_x(c + 1, i // 2)
+                if i % 2 == 1 and 0 < c < N_CHUNKS - 1:
+                    quantise_x(c + 1, i // 2)
             if c == 0:
                 for n in range(PHASES):
                     transpose_x(1, n)
@@ -404,6 +410,8 @@ def tile_maskmlp_pa_kernel(tc, x, wes1, wes2, wes3, bias1, bias2, bias3, out):
             if c + 1 < N_CHUNKS:
                 for jt in range(J_TILES):
                     last_term(c + 1, jt)
+        regroup(N_CHUNKS * PHASES - 1)
+        quantise_g(N_CHUNKS - 1, 1)
         for n in range(2 * PHASES):
             second_layer(N_CHUNKS - 1, n)
             finish(N_CHUNKS - 1, n)

@@ -284,53 +284,6 @@ def tile_maskmlp_pa_kernel(tc, x, wes1, wes2, wes3, bias1, bias2, bias3, out):
                 out=w2_codes[:, i, :].bitcast(FP8X4), scales=w2_scales[:, i, :], in_=w2_grouped[i][:]
             )
 
-        rows_j = const.tile([P, P], BF16)
-        nc.vector.memset(rows_j[:], 0.0)
-        nc.sync.dma_start(out=rows_j[0:16, :], in_=bias2.rearrange("(a m) -> a m", m=P))
-        nc.sync.dma_start(out=rows_j[16:20, :], in_=bias3.rearrange("(a m) -> a m", m=P))
-        rows_h = const.tile([P, 2 * P], BF16)
-        nc.vector.memset(rows_h[:], 0.0)
-        nc.sync.dma_start(out=rows_h[0:8, :], in_=bias1.rearrange("(a m) -> a m", m=2 * P))
-
-        pitch = WIDTH + PHASES
-        wes3_flat = wes3.rearrange("a b -> (a b)")
-        w3_bf16 = const.tile([P, J_TILES, 16], BF16)
-        for jt in range(J_TILES):
-            lead = WIDTH if jt == J_TILES - 1 else 0
-            first = jt * P * pitch - lead
-            window = wes3_flat[first : first + P * pitch].rearrange("(p c) -> p c", c=pitch)
-            nc.sync.dma_start(out=w3_bf16[:, jt, 0:PHASES], in_=window[:, lead : lead + PHASES])
-
-        w3 = const.tile([P, J_TILES, PHASES], F32)
-        b1 = const.tile([P, 16], F32)
-        b2_b3 = const.tile([P, 20], F32)
-        b23 = const.tile([P, PHASES, J_TILES], F32)
-        diag = const.tile([P, J_TILES, TENSOR_TERMS, P], BF16)
-        def prepare_small():
-            nc.vector.tensor_copy(out=w3[:], in_=w3_bf16[:, :, 0:PHASES])
-            cols_h = bank("rest", [P, P])
-            nc.tensor.transpose(cols_h[:], rows_h[:].bitcast(F32), ident_f32[:])
-            nc.vector.tensor_copy(out=b1[:], in_=cols_h[:, 0:8].bitcast(BF16))
-            cols_j = bank("rest", [P, P], BF16)
-            nc.tensor.transpose(cols_j[:], rows_j[:], ident_bf16[:])
-            nc.vector.tensor_copy(out=b2_b3[:], in_=cols_j[:, 0:20])
-            nc.vector.tensor_tensor(
-                out=b23[:],
-                in0=b2_b3[:, 0:16].rearrange("p (i t) -> p i t", i=PHASES),
-                in1=b2_b3[:, 16:20].unsqueeze(1).to_broadcast([P, PHASES, J_TILES]),
-                op=ALU.add,
-            )
-            for jt in range(J_TILES):
-                for k in range(TENSOR_TERMS):
-                    nc.vector.tensor_scalar(
-                        out=diag[:, jt, k, :],
-                        in0=ident_bf16[:],
-                        scalar1=w3[:, jt, k : k + 1],
-                        scalar2=0.0,
-                        op0=ALU.mult,
-                        op1=ALU.add,
-                    )
-
         w1_view = wes1.rearrange("(a m e) c -> a e m c", a=2, e=2)
         w1_pairs = [
             grouped.tile([P, 2, HID, PACK], BF16, name="w1_pair%d" % u, bufs=1, align_bytes=64) for u in range(2)
@@ -343,8 +296,6 @@ def tile_maskmlp_pa_kernel(tc, x, wes1, wes2, wes3, bias1, bias2, bias3, out):
                 nc.sync.dma_start(out=w1_sb[:, part], in_=w1_view[t // 2, t % 2][:, part])
             for u in range(2):
                 store_pair(transpose_pair(w1_sb, u, ("first", "second")[u]), w1_pairs[u], t * P, u == 1)
-            if t == 0:
-                prepare_small()
         for rl in range(ROW_TILES):
             load_x(rl)
         quantise_pair(w1_pairs[0], 0, w1_codes, w1_scales)
@@ -354,6 +305,52 @@ def tile_maskmlp_pa_kernel(tc, x, wes1, wes2, wes3, bias1, bias2, bias3, out):
         quantise_x(0, 0)
         quantise_pair(w1_pairs[1], 1, w1_codes, w1_scales)
 
+        rows_j = const.tile([P, P], BF16)
+        nc.vector.memset(rows_j[:], 0.0)
+        nc.sync.dma_start(out=rows_j[0:16, :], in_=bias2.rearrange("(a m) -> a m", m=P))
+        nc.sync.dma_start(out=rows_j[16:20, :], in_=bias3.rearrange("(a m) -> a m", m=P))
+        rows_h = const.tile([P, 2 * P], BF16)
+        nc.vector.memset(rows_h[:], 0.0)
+        nc.sync.dma_start(out=rows_h[0:8, :], in_=bias1.rearrange("(a m) -> a m", m=2 * P))
+
+        pitch = WIDTH + PHASES
+        wes3_flat = wes3.rearrange("a b -> (a b)")
+        w3_bf16 = const.tile([P, J_TILES, 16], BF16)
+        lead = WIDTH
+        body = wes3_flat[0 : (J_TILES - 1) * P * pitch].rearrange("(t p c) -> p t c", p=P, c=pitch)
+        nc.sync.dma_start(out=w3_bf16[:, 0 : J_TILES - 1, 0:PHASES], in_=body[:, :, 0:PHASES])
+        first = (J_TILES - 1) * P * pitch - lead
+        tail = wes3_flat[first : first + P * pitch].rearrange("(p c) -> p c", c=pitch)
+        nc.sync.dma_start(out=w3_bf16[:, J_TILES - 1, 0:PHASES], in_=tail[:, lead : lead + PHASES])
+
+        w3 = const.tile([P, J_TILES, PHASES], F32)
+        nc.vector.tensor_copy(out=w3[:], in_=w3_bf16[:, :, 0:PHASES])
+        cols_h = bank("rest", [P, P])
+        nc.tensor.transpose(cols_h[:], rows_h[:].bitcast(F32), ident_f32[:])
+        b1 = const.tile([P, 16], F32)
+        nc.vector.tensor_copy(out=b1[:], in_=cols_h[:, 0:8].bitcast(BF16))
+        cols_j = bank("rest", [P, P], BF16)
+        nc.tensor.transpose(cols_j[:], rows_j[:], ident_bf16[:])
+        b2_b3 = const.tile([P, 20], F32)
+        nc.vector.tensor_copy(out=b2_b3[:], in_=cols_j[:, 0:20])
+        b23 = const.tile([P, PHASES, J_TILES], F32)
+        nc.vector.tensor_tensor(
+            out=b23[:],
+            in0=b2_b3[:, 0:16].rearrange("p (i t) -> p i t", i=PHASES),
+            in1=b2_b3[:, 16:20].unsqueeze(1).to_broadcast([P, PHASES, J_TILES]),
+            op=ALU.add,
+        )
+        diag = const.tile([P, J_TILES, TENSOR_TERMS, P], BF16)
+        for jt in range(J_TILES):
+            for k in range(TENSOR_TERMS):
+                nc.vector.tensor_scalar(
+                    out=diag[:, jt, k, :],
+                    in0=ident_bf16[:],
+                    scalar1=w3[:, jt, k : k + 1],
+                    scalar2=0.0,
+                    op0=ALU.mult,
+                    op1=ALU.add,
+                )
         for row_tile in range(ROW_TILES, 2 * ROW_TILES):
             load_x(row_tile)
         for i in range(PHASES):

@@ -27,7 +27,7 @@ BANK = 512
 TENSOR_TERMS = 3
 PAIR = 2 * CHUNK
 VECTOR_ROWS = (256, 128, 0, 0)
-BANKS = {"first": 2, "second": 2, "side": 2, "rest": 2}
+BANKS = {"first": 2, "second": 2, "side": 4}
 
 FLOPS = 2 * 2 * PHASES * ROWS * SEG * HID
 BYTES = 2 * (ROWS * WIDTH + HID * WIDTH + PHASES * SEG * HID) + 4 * ROWS * WIDTH
@@ -133,7 +133,7 @@ def tile_maskmlp_pa_kernel(tc, x, wes1, wes2, wes3, bias1, bias2, bias3, out):
 
         def sum_residual(c, rl):
             rows = slice(rl * P, (rl + 1) * P)
-            r_ps = bank("rest", [P, J_TILES, P])
+            r_ps = bank("side", [P, J_TILES, P])
             for jt in range(J_TILES):
                 for k in range(TENSOR_TERMS):
                     u, e = divmod(k, 2)
@@ -325,11 +325,11 @@ def tile_maskmlp_pa_kernel(tc, x, wes1, wes2, wes3, bias1, bias2, bias3, out):
 
         w3 = const.tile([P, J_TILES, PHASES], F32)
         nc.vector.tensor_copy(out=w3[:], in_=w3_bf16[:, :, 0:PHASES])
-        cols_h = bank("rest", [P, P])
+        cols_h = bank("side", [P, P])
         nc.tensor.transpose(cols_h[:], rows_h[:].bitcast(F32), ident_f32[:])
         b1 = const.tile([P, 16], F32)
         nc.vector.tensor_copy(out=b1[:], in_=cols_h[:, 0:8].bitcast(BF16))
-        cols_j = bank("rest", [P, P], BF16)
+        cols_j = bank("side", [P, P], BF16)
         nc.tensor.transpose(cols_j[:], rows_j[:], ident_bf16[:])
         b2_b3 = const.tile([P, 20], F32)
         nc.vector.tensor_copy(out=b2_b3[:], in_=cols_j[:, 0:20])
@@ -361,7 +361,7 @@ def tile_maskmlp_pa_kernel(tc, x, wes1, wes2, wes3, bias1, bias2, bias3, out):
         bias = const.tile([P, J_TILES, P, PHASES], F32)
 
         def spread_bias(jt):
-            b_ps = bank("rest", [P, PHASES, P])
+            b_ps = bank("side", [P, PHASES, P])
             for i in range(PHASES):
                 nc.tensor.transpose(b_ps[:, i, :], b23[:, i, jt : jt + 1].to_broadcast([P, P]), ident_f32[:])
             nc.vector.tensor_copy(out=bias[:, jt, :, :], in_=b_ps[:].rearrange("p i j -> p j i"))
@@ -377,7 +377,8 @@ def tile_maskmlp_pa_kernel(tc, x, wes1, wes2, wes3, bias1, bias2, bias3, out):
         for c in range(N_CHUNKS):
             for i in range(PHASES):
                 s = PHASES * c + i
-                first_layer(s)
+                with tc.high_priority(offset=40):
+                    first_layer(s)
                 gelu(s)
                 if c + 1 < N_CHUNKS and c > 0:
                     transpose_x(c + 1, i)

from contextlib import ExitStack

import concourse.mybir as mybir
from concourse.masks import make_identity

F32 = mybir.dt.float32
BF16 = mybir.dt.bfloat16
U32 = mybir.dt.uint32
U8 = mybir.dt.uint8
FP8X4 = mybir.dt.float8_e4m3fn_x4
ACT = mybir.ActivationFunctionType
ALU = mybir.AluOpType

P = 128
PACK = 4
PHASES = 4
SEG = 512
HID = 512
ROWS = 1024
WIDTH = PHASES * SEG
CHUNK = 256
N_CHUNKS = ROWS // CHUNK
ROW_TILES = CHUNK // P
J_TILES = SEG // P
H_TILES = HID // P
BANK = 512
TENSOR_TERMS = 3
PAIR = 2 * CHUNK
VECTOR_ROWS = (256, 128, 0, 0)
BANKS = {"first": 2, "second": 2, "side": 4}

FLOPS = 2 * 2 * PHASES * ROWS * SEG * HID
BYTES = 2 * (ROWS * WIDTH + HID * WIDTH + PHASES * SEG * HID) + 4 * ROWS * WIDTH


def tile_maskmlp_pa_kernel(tc, x, wes1, wes2, wes3, bias1, bias2, bias3, out):
    nc = tc.nc
    x_rows = x.flatten_outer_dims()
    out_rows = out.flatten_outer_dims()

    with ExitStack() as ctx:
        const = ctx.enter_context(tc.tile_pool(name="const", bufs=1))
        load = ctx.enter_context(tc.tile_pool(name="load", bufs=10))
        grouped = ctx.enter_context(tc.tile_pool(name="grouped", bufs=4))
        keep = ctx.enter_context(tc.tile_pool(name="keep", bufs=1))
        work = ctx.enter_context(tc.tile_pool(name="work", bufs=2))
        psum = ctx.enter_context(tc.psum_pool(name="psum", bufs=2))

        ident_f32 = const.tile([P, P], F32)
        make_identity(nc, ident_f32[:])
        ident_bf16 = const.tile([P, P], BF16)
        make_identity(nc, ident_bf16[:])

        warm = const.tile([P, 2], F32)
        nc.vector.memset(warm[:], 0.0)
        nc.scalar.activation(out=warm[:, 1:2], in_=warm[:, 0:1], func=ACT.Gelu)

        w1_codes = keep.tile([P, PHASES, HID], U32, align_bytes=64)
        w1_scales = keep.tile([P, PHASES, HID], U8, align_bytes=64)
        w2_codes = keep.tile([P, PHASES, SEG], U32, align_bytes=64)
        w2_scales = keep.tile([P, PHASES, SEG], U8, align_bytes=64)

        def bank(tag, shape, dtype=F32, name=None):
            return psum.tile(shape, dtype, tag=tag, bufs=BANKS[tag], name=name or tag)

        def empty_bank(on_vector, dst, src):
            if on_vector:
                nc.vector.tensor_copy(out=dst, in_=src)
            else:
                nc.scalar.copy(out=dst, in_=src)

        def transpose_pair(rows_sb, u, tag):
            words = rows_sb[:].bitcast(F32).rearrange("r (j u) -> r u j", u=2)
            w_ps = bank(tag, [P, BANK])
            for jt in range(J_TILES):
                nc.tensor.transpose(
                    w_ps[:, jt * P : (jt + 1) * P], words[:, u, jt * P : (jt + 1) * P], ident_f32[:]
                )
            return w_ps

        def store_pair(w_ps, pair_tile, first_row, on_vector):
            empty_bank(
                on_vector,
                pair_tile[:, :, first_row : first_row + P, :],
                w_ps[:].bitcast(BF16).rearrange("p (t r e) -> p e r t", t=J_TILES, e=2),
            )

        def quantise_pair(pair_tile, u, codes, scales):
            nc.vector.quantize_mx(
                out=codes[:, 2 * u : 2 * u + 2, :].rearrange("p e r -> p (e r)").bitcast(FP8X4),
                scales=scales[:, 2 * u : 2 * u + 2, :].rearrange("p e r -> p (e r)"),
                in_=pair_tile[:].rearrange("p e r t -> p (e r t)"),
            )

        x_sb, x_ps, x_pairs, x_codes, x_scales, term, big_r = {}, {}, {}, {}, {}, {}, {}
        a_ps, g, g_grouped, g_codes, g_scales, m_ps, o_sb = {}, {}, {}, {}, {}, {}, {}

        def load_x(row_tile):
            x_sb[row_tile] = load.tile([P, WIDTH], BF16, tag="rows", name="x_sb")
            nc.sync.dma_start(out=x_sb[row_tile][:], in_=x_rows[row_tile * P : (row_tile + 1) * P, :])

        def new_x(c):
            x_pairs[c] = [
                grouped.tile([P, 2, CHUNK, PACK], BF16, name="x_pair", tag="x_pair", align_bytes=64) for u in range(2)
            ]
            x_codes[c] = keep.tile([P, PHASES, CHUNK], U32, name="x_codes%d" % c, align_bytes=64)
            x_scales[c] = keep.tile([P, PHASES, CHUNK], U8, name="x_scales%d" % c, align_bytes=64)

        def transpose_x(c, n):
            u, rl = divmod(n, ROW_TILES)
            if n == 0:
                new_x(c)
            x_ps[c, n] = transpose_pair(x_sb[c * ROW_TILES + rl], u, "side")

        def store_x(c, n, on_vector):
            u, rl = divmod(n, ROW_TILES)
            store_pair(x_ps[c, n], x_pairs[c][u], rl * P, on_vector)

        def quantise_x(c, u):
            quantise_pair(x_pairs[c][u], u, x_codes[c], x_scales[c])

        def last_term(c, jt):
            if jt == 0:
                term[c] = work.tile([P, J_TILES, CHUNK], F32, name="term")
            nc.vector.tensor_scalar(
                out=term[c][:, jt, :],
                in0=x_pairs[c][1][:, 1, :, jt],
                scalar1=w3[:, jt, 3:4],
                scalar2=0.0,
                op0=ALU.mult,
                op1=ALU.add,
            )

        def sum_residual(c, rl):
            rows = slice(rl * P, (rl + 1) * P)
            r_ps = bank("side", [P, J_TILES, P])
            for jt in range(J_TILES):
                for k in range(TENSOR_TERMS):
                    u, e = divmod(k, 2)
                    nc.tensor.matmul(
                        out=r_ps[:, jt, :],
                        lhsT=x_pairs[c][u][:, e, rows, jt],
                        rhs=diag[:, jt, k, :],
                        start=(k == 0),
                        stop=False,
                    )
                nc.tensor.matmul(
                    out=r_ps[:, jt, :],
                    lhsT=term[c][:, jt, rows],
                    rhs=ident_f32[:],
                    is_transpose=True,
                    start=False,
                    stop=True,
                )
            return r_ps

        def add_bias(c, rl, r_ps):
            row_tile = c * ROW_TILES + rl
            big_r[row_tile] = work.tile([P, J_TILES, P, PHASES], F32, name="big_r", bufs=4)
            nc.vector.tensor_tensor(
                out=big_r[row_tile][:],
                in0=bias[:],
                in1=r_ps[:].unsqueeze(3).to_broadcast([P, J_TILES, P, PHASES]),
                op=ALU.add,
            )

        def first_layer(s):
            c, i = divmod(s, PHASES)
            a_ps[s] = [bank("first", [P, 2, CHUNK]) for half in range(2)]
            for t in range(H_TILES):
                nc.tensor.matmul_mx(
                    out=a_ps[s][t // 2][:, t % 2, :],
                    lhsT=w1_codes[:, i, t * P : (t + 1) * P].bitcast(FP8X4),
                    lhsT_scale=w1_scales[:, i, t * P : (t + 1) * P],
                    rhs=x_codes[c][:, i, :].bitcast(FP8X4),
                    rhs_scale=x_scales[c][:, i, :],
                    start=True,
                    stop=True,
                )

        def gelu(s):
            i = s % PHASES
            g[s] = work.tile([P, H_TILES, CHUNK], BF16, name="g", bufs=3)
            for t in range(H_TILES):
                nc.scalar.activation(
                    out=g[s][:, t, :],
                    in_=a_ps[s][t // 2][:, t % 2, :],
                    func=ACT.Gelu,
                    bias=b1[:, i * H_TILES + t : i * H_TILES + t + 1],
                    scale=1.0,
                )

        def regroup(s):
            c, i = divmod(s, PHASES)
            u, e = divmod(i, 2)
            if e == 0:
                g_grouped[c, u] = work.tile([P, PAIR, PACK], BF16, name="g_grouped", bufs=2, align_bytes=64)
            dst = g_grouped[c, u][:, e * CHUNK : (e + 1) * CHUNK, :]
            split = VECTOR_ROWS[c]
            for on_vector, rows in ((True, slice(0, split)), (False, slice(split, CHUNK))):
                if rows.start < rows.stop:
                    empty_bank(
                        on_vector,
                        dst[:, rows, :].rearrange("p (c n) t -> p c t n", n=4),
                        g[s][:, :, rows].rearrange("p t (c n) -> p c t n", n=4),
                    )

        def quantise_g(c, u):
            g_codes[c, u] = work.tile([P, PAIR], U32, name="g_codes%d" % u, align_bytes=64)
            g_scales[c, u] = work.tile([P, PAIR], U8, name="g_scales%d" % u, align_bytes=64)
            nc.vector.quantize_mx(
                out=g_codes[c, u][:].bitcast(FP8X4),
                scales=g_scales[c, u][:],
                in_=g_grouped[c, u][:].rearrange("p r t -> p (r t)"),
            )

        def second_layer(c, n):
            rl, jt = divmod(n, J_TILES)
            m_ps[c, n] = bank(("second", "first")[n % 2 if c == N_CHUNKS - 1 else 0], [P, PHASES, P])
            for i in range(PHASES):
                u, e = divmod(i, 2)
                cols = slice(e * CHUNK + rl * P, e * CHUNK + (rl + 1) * P)
                nc.tensor.matmul_mx(
                    out=m_ps[c, n][:, i, :],
                    lhsT=g_codes[c, u][:, cols].bitcast(FP8X4),
                    lhsT_scale=g_scales[c, u][:, cols],
                    rhs=w2_codes[:, i, jt * P : (jt + 1) * P].bitcast(FP8X4),
                    rhs_scale=w2_scales[:, i, jt * P : (jt + 1) * P],
                    start=True,
                    stop=True,
                )

        def finish(c, n):
            rl, jt = divmod(n, J_TILES)
            row_tile = c * ROW_TILES + rl
            if jt == 0:
                o_sb[row_tile] = work.tile([P, J_TILES, P, PHASES], F32, name="o_sb", bufs=3)
            nc.vector.tensor_tensor(
                out=o_sb[row_tile][:, jt, :, :],
                in0=m_ps[c, n][:].rearrange("p i j -> p j i"),
                in1=big_r[row_tile][:, jt, :, :],
                op=ALU.add,
            )
            banks = 1 if row_tile == ROWS // P - 1 else 2
            if (jt + 1) % banks == 0:
                tiles = slice(jt + 1 - banks, jt + 1)
                nc.sync.dma_start(
                    out=out_rows[row_tile * P : (row_tile + 1) * P, tiles.start * BANK : tiles.stop * BANK],
                    in_=o_sb[row_tile][:, tiles, :, :].rearrange("p t j i -> p (t j i)"),
                )

        def load_w2(i):
            w2_sb[i] = load.tile([P, WIDTH], BF16, tag="rows", name="w2_sb")
            block = wes2[i * SEG : (i + 1) * SEG, i * HID : (i + 1) * HID]
            nc.sync.dma_start(
                out=w2_sb[i][:].rearrange("p (t h) -> p t h", t=J_TILES),
                in_=block.rearrange("(t p) h -> p t h", p=P),
            )

        w2_sb, w2_grouped = {}, {}

        def transpose_w2(i, half):
            words = w2_sb[i][:].bitcast(F32)
            w_ps = bank("side", [P, BANK])
            for a in range(2):
                for jl in range(2):
                    src = (2 * half + jl) * (HID // 2) + a * P
                    dst = (2 * a + jl) * P
                    nc.tensor.transpose(w_ps[:, dst : dst + P], words[:, src : src + P], ident_f32[:])
            return w_ps

        def store_w2(i, half, w_ps):
            if half == 0:
                w2_grouped[i] = work.tile([P, SEG * PACK], BF16, name="w2_grouped", align_bytes=64)
            nc.scalar.copy(
                out=w2_grouped[i][:].bitcast(F32)[:, half * BANK : (half + 1) * BANK].rearrange(
                    "p (j a) -> p j a", a=2
                ),
                in_=w_ps[:].rearrange("p (a j) -> p j a", a=2),
            )

        def quantise_w2(i):
            nc.vector.quantize_mx(
                out=w2_codes[:, i, :].bitcast(FP8X4), scales=w2_scales[:, i, :], in_=w2_grouped[i][:]
            )

        w1_view = wes1.rearrange("(a m e) c -> a e m c", a=2, e=2)
        w1_pairs = [
            grouped.tile([P, 2, HID, PACK], BF16, name="w1_pair%d" % u, bufs=1, align_bytes=64) for u in range(2)
        ]
        for t in range(H_TILES):
            w1_sb = load.tile([P, WIDTH], BF16, tag="rows", name="w1_sb")
            pieces = J_TILES if t == 0 else 1
            for cut in range(pieces):
                part = slice(cut * WIDTH // pieces, (cut + 1) * WIDTH // pieces)
                nc.sync.dma_start(out=w1_sb[:, part], in_=w1_view[t // 2, t % 2][:, part])
            for u in range(2):
                store_pair(transpose_pair(w1_sb, u, ("first", "second")[u]), w1_pairs[u], t * P, u == 1)
        for rl in range(ROW_TILES):
            load_x(rl)
        quantise_pair(w1_pairs[0], 0, w1_codes, w1_scales)
        for n in range(ROW_TILES):
            transpose_x(0, n)
            store_x(0, n, False)
        quantise_x(0, 0)
        quantise_pair(w1_pairs[1], 1, w1_codes, w1_scales)

        rows_j = const.tile([P, P], BF16)
        nc.vector.memset(rows_j[:], 0.0)
        nc.sync.dma_start(out=rows_j[0:16, :], in_=bias2.rearrange("(a m) -> a m", m=P))
        nc.sync.dma_start(out=rows_j[16:20, :], in_=bias3.rearrange("(a m) -> a m", m=P))
        rows_h = const.tile([P, 2 * P], BF16)
        nc.vector.memset(rows_h[:], 0.0)
        nc.sync.dma_start(out=rows_h[0:8, :], in_=bias1.rearrange("(a m) -> a m", m=2 * P))

        pitch = WIDTH + PHASES
        wes3_flat = wes3.rearrange("a b -> (a b)")
        w3_bf16 = const.tile([P, J_TILES, 16], BF16)
        lead = WIDTH
        body = wes3_flat[0 : (J_TILES - 1) * P * pitch].rearrange("(t p c) -> p t c", p=P, c=pitch)
        nc.sync.dma_start(out=w3_bf16[:, 0 : J_TILES - 1, 0:PHASES], in_=body[:, :, 0:PHASES])
        first = (J_TILES - 1) * P * pitch - lead
        tail = wes3_flat[first : first + P * pitch].rearrange("(p c) -> p c", c=pitch)
        nc.sync.dma_start(out=w3_bf16[:, J_TILES - 1, 0:PHASES], in_=tail[:, lead : lead + PHASES])

        w3 = const.tile([P, J_TILES, PHASES], F32)
        nc.vector.tensor_copy(out=w3[:], in_=w3_bf16[:, :, 0:PHASES])
        cols_h = bank("side", [P, P])
        nc.tensor.transpose(cols_h[:], rows_h[:].bitcast(F32), ident_f32[:])
        b1 = const.tile([P, 16], F32)
        nc.vector.tensor_copy(out=b1[:], in_=cols_h[:, 0:8].bitcast(BF16))
        cols_j = bank("side", [P, P], BF16)
        nc.tensor.transpose(cols_j[:], rows_j[:], ident_bf16[:])
        b2_b3 = const.tile([P, 20], F32)
        nc.vector.tensor_copy(out=b2_b3[:], in_=cols_j[:, 0:20])
        b23 = const.tile([P, PHASES, J_TILES], F32)
        nc.vector.tensor_tensor(
            out=b23[:],
            in0=b2_b3[:, 0:16].rearrange("p (i t) -> p i t", i=PHASES),
            in1=b2_b3[:, 16:20].unsqueeze(1).to_broadcast([P, PHASES, J_TILES]),
            op=ALU.add,
        )
        diag = const.tile([P, J_TILES, TENSOR_TERMS, P], BF16)
        for jt in range(J_TILES):
            for k in range(TENSOR_TERMS):
                nc.vector.tensor_scalar(
                    out=diag[:, jt, k, :],
                    in0=ident_bf16[:],
                    scalar1=w3[:, jt, k : k + 1],
                    scalar2=0.0,
                    op0=ALU.mult,
                    op1=ALU.add,
                )
        for row_tile in range(ROW_TILES, 2 * ROW_TILES):
            load_x(row_tile)
        for i in range(PHASES):
            load_w2(i)
        for row_tile in range(2 * ROW_TILES, ROWS // P):
            load_x(row_tile)

        bias = const.tile([P, J_TILES, P, PHASES], F32)

        def spread_bias(jt):
            b_ps = bank("side", [P, PHASES, P])
            for i in range(PHASES):
                nc.tensor.transpose(b_ps[:, i, :], b23[:, i, jt : jt + 1].to_broadcast([P, P]), ident_f32[:])
            nc.vector.tensor_copy(out=bias[:, jt, :, :], in_=b_ps[:].rearrange("p i j -> p j i"))

        for n in range(ROW_TILES, 2 * ROW_TILES):
            transpose_x(0, n)
            store_x(0, n, False)
        quantise_x(0, 1)
        for jt in range(J_TILES):
            spread_bias(jt)
        for jt in range(J_TILES):
            last_term(0, jt)
        for c in range(N_CHUNKS):
            for i in range(PHASES):
                s = PHASES * c + i
                with tc.high_priority(offset=40):
                    first_layer(s)
                gelu(s)
                if c + 1 < N_CHUNKS and c > 0:
                    transpose_x(c + 1, i)
                    store_x(c + 1, i, False)
                if c == 0:
                    for half in range(2):
                        store_w2(i, half, transpose_w2(i, half))
                    quantise_w2(i)
                if s > 0:
                    regroup(s - 1)
                if s >= 2 and s % 2 == 0:
                    quantise_g((s - 2) // PHASES, (s - 2) % PHASES // 2)
                if c > 0:
                    for n in range(2 * i, 2 * i + 2):
                        second_layer(c - 1, n)
                        finish(c - 1, n)
                if i < ROW_TILES:
                    add_bias(c, i, sum_residual(c, i))
                if i % 2 == 1 and 0 < c < N_CHUNKS - 1:
                    quantise_x(c + 1, i // 2)
            if c == 0:
                for n in range(PHASES):
                    transpose_x(1, n)
                    store_x(1, n, False)
                    if n % 2 == 1:
                        quantise_x(1, n // 2)
            if c + 1 < N_CHUNKS:
                for jt in range(J_TILES):
                    last_term(c + 1, jt)
        regroup(N_CHUNKS * PHASES - 1)
        quantise_g(N_CHUNKS - 1, 1)
        for n in range(2 * PHASES):
            second_layer(N_CHUNKS - 1, n)
            finish(N_CHUNKS - 1, n)
